import numpy as np
import ml_dtypes


def mxq(x, axis, fmt="e4m3"):
    dtype, down = {"e4m3": (ml_dtypes.float8_e4m3fn, 7), "e5m2": (ml_dtypes.float8_e5m2, 14)}[fmt]
    v = np.moveaxis(np.asarray(x, np.float32).astype(ml_dtypes.bfloat16).astype(np.float64), axis, -1)
    blocks = v.reshape(v.shape[:-1] + (-1, 32))
    amax = np.abs(blocks).max(-1, keepdims=True)
    byte = np.maximum(np.where(amax > 0, np.frexp(amax)[1] - 1 + 127, 0) - down, 1)
    scale = np.exp2(byte - 127.0)
    codes = (blocks / scale).astype(np.float32).astype(dtype).astype(np.float64)
    return np.moveaxis((codes * scale).reshape(v.shape), -1, axis)


WIDE = False


def mx_kscale(k):
    if not WIDE:
        return np.ones(k)
    levels = np.array([10, -10, 5, -5, 0])
    a = np.random.permutation(np.resize(levels, k // 512 * 4)).reshape(k // 512, 4)
    idx = np.arange(k)
    return np.exp2(a[idx // 512, idx % 128 // 32])


BF16 = ml_dtypes.bfloat16


def bf(x):
    return np.asarray(x, np.float32).astype(BF16)


def f64(x):
    return np.asarray(x).astype(np.float64)


E2M1 = np.array([0.0, 0.5, 1.0, 1.5, 2.0, 3.0, 4.0, 6.0, -0.0, -0.5, -1.0, -1.5, -2.0, -3.0, -4.0, -6.0])


def pack_weight(w, fmt):
    k, n = w.shape
    w = f64(bf(w)).reshape(k // 32, 32, n)
    amax = np.abs(w).max(1)
    if fmt == "e4m3":
        byte = np.frexp(amax)[1] - 1 + 127 - 7
    else:
        mant, ex = np.frexp(amax / 6.0)
        byte = np.where(mant > 0.5, ex, ex - 1) + 127
    byte = np.clip(np.where(amax > 0, byte, 1), 1, 254)
    scaled = (w * np.exp2(127.0 - byte)[:, None, :]).reshape(k, n).astype(np.float32)
    by_word = np.ascontiguousarray(scaled.reshape(k // 512, 128, 4, n).transpose(0, 1, 3, 2))
    if fmt == "e4m3":
        words = by_word.astype(ml_dtypes.float8_e4m3fn).view(np.uint8)
    else:
        c = by_word.astype(ml_dtypes.float4_e2m1fn).view(np.uint8) & 0xF
        words = c[..., 0::2] | (c[..., 1::2] << 4)
    return np.ascontiguousarray(words), np.ascontiguousarray(byte.astype(np.uint8).reshape(k // 512, 16, n))


def unpack_weight(words, scales, fmt):
    g, p, n, _ = words.shape
    if fmt == "e4m3":
        vals = np.ascontiguousarray(words).view(ml_dtypes.float8_e4m3fn).astype(np.float64)
    else:
        nib = np.empty((g, p, n, 4), np.uint8)
        nib[..., 0::2] = words & 0xF
        nib[..., 1::2] = words >> 4
        vals = E2M1[nib]
    vals = vals * np.repeat(np.exp2(scales.astype(np.float64) - 127.0), 8, axis=1)[..., None]
    return vals.transpose(0, 1, 3, 2).reshape(g * 512, n)


B, D = 1024, 128


def setup_inputs():
    a = mx_kscale(D * D)[::D]
    c = np.concatenate((a, np.ones(D)))
    hspatial = bf(np.random.standard_normal((B, D)) * a)
    htext = bf(np.random.standard_normal((B, D)))
    W_L = bf(np.random.standard_normal((2 * D, 2 * D)) / np.sqrt(2 * D) / c)
    b_L = bf(np.random.standard_normal(2 * D) * 0.3)
    w2 = np.random.standard_normal((2 * D, D * D)) / D / np.repeat(a, D)
    words, scales = pack_weight(np.ascontiguousarray(w2.T), "e4m3")
    b_L2 = bf(np.random.standard_normal(2 * D) * 0.3)
    return {"hspatial": hspatial,
            "htext": htext,
            "W_L": W_L,
            "b_L": b_L,
            "W_L2_words": words,
            "W_L2_scales": scales,
            "b_L2": b_L2}


def reference(hspatial, htext, W_L, b_L, W_L2_words, W_L2_scales, b_L2):
    hs, ht = f64(hspatial), f64(htext)
    g = np.concatenate((hs, ht), axis=1) @ f64(W_L).T + f64(b_L)
    v = (hs[:, :, None] * ht[:, None, :]).reshape(hs.shape[0], -1)
    u = (mxq(v, 1, "e4m3") @ unpack_weight(W_L2_words, W_L2_scales, "e4m3")) + f64(b_L2)
    return np.concatenate((g, u), axis=1)

@@ -1,0 +1,243 @@
+from contextlib import ExitStack
+
+import concourse.mybir as mybir
+from concourse.masks import make_identity
+
+BF16 = mybir.dt.bfloat16
+F32 = mybir.dt.float32
+I32 = mybir.dt.int32
+U32 = mybir.dt.uint32
+U8 = mybir.dt.uint8
+FP8X4 = mybir.dt.float8_e4m3fn_x4
+
+P = 128
+BATCH = 1024
+FEATURES = 128
+WIDTH = 256
+PACK = 4
+BLOCK_P = 8
+I_PER_PASS = P // BLOCK_P
+I_GROUPS = FEATURES // I_PER_PASS
+J_BLOCKS = FEATURES // (BLOCK_P * PACK)
+B_TILES = BATCH // P
+HALVES = 2
+TILES_PER_HALF = B_TILES // HALVES
+HALF_B = TILES_PER_HALF * P
+STEPS = HALVES * J_BLOCKS * I_GROUPS
+
+FLOPS = 2 * BATCH * FEATURES * FEATURES * WIDTH + 2 * BATCH * 2 * FEATURES * WIDTH
+
+
+def place_of(step):
+    half, rest = divmod(step, J_BLOCKS * I_GROUPS)
+    jb, ig = divmod(rest, I_GROUPS)
+    return half, jb, ig
+
+
+def tile_deepandwide_kernel(
+    tc, hspatial, htext, W_L, b_L, W_L2_words, W_L2_scales, b_L2, out
+):
+    nc = tc.nc
+    with ExitStack() as ctx:
+        keep = ctx.enter_context(tc.tile_pool(name="keep", bufs=1))
+        spread = ctx.enter_context(tc.tile_pool(name="spread", bufs=2))
+        stream = ctx.enter_context(tc.tile_pool(name="stream", bufs=3))
+        psum_acc = ctx.enter_context(tc.psum_pool(name="psum_acc", bufs=1))
+        psum_work = ctx.enter_context(tc.psum_pool(name="psum_work", bufs=4))
+
+        ident_f32 = keep.tile([P, P], F32)
+        make_identity(nc, ident_f32[:])
+        ident_bf16 = keep.tile([P, P], BF16)
+        make_identity(nc, ident_bf16[:])
+        ones = keep.tile([P, P], BF16)
+        nc.gpsimd.memset(ones[:], 1.0)
+
+        ht_sb = keep.tile([P, B_TILES, FEATURES], BF16)
+        nc.sync.dma_start(out=ht_sb[:], in_=htext.rearrange("(c n) j -> c n j", n=B_TILES))
+        hs_sb = keep.tile([P, B_TILES, FEATURES], BF16)
+        nc.sync.dma_start(out=hs_sb[:], in_=hspatial.rearrange("(c n) i -> c n i", n=B_TILES))
+
+        w_scales = keep.tile([P, I_GROUPS, J_BLOCKS, WIDTH], U8, align_bytes=64)
+        nc.vector.memset(w_scales[:].rearrange("p a b n -> p (a b n)").bitcast(I32), 0)
+        scale_rows = (
+            W_L2_scales.rearrange("g q n -> (g q) n")
+            .rearrange("(ig Q r jb) n -> Q r ig (jb n)", ig=I_GROUPS, Q=4, r=4, jb=J_BLOCKS)
+            .bitcast(I32)
+        )
+        for Q in range(4):
+            nc.sync.dma_start(
+                out=w_scales[32 * Q : 32 * Q + 4].rearrange("r a b n -> r a (b n)").bitcast(I32),
+                in_=scale_rows[Q],
+            )
+
+        w_words = keep.tile([P, J_BLOCKS, I_GROUPS, WIDTH], U32, align_bytes=64)
+        word_rows = (
+            W_L2_words.rearrange("g p n t -> (g p) (n t)")
+            .bitcast(I32)
+            .rearrange("(ig s jb w) x -> ig jb s w x", ig=I_GROUPS, s=I_PER_PASS, jb=J_BLOCKS, w=BLOCK_P)
+        )
+        for jb in range(J_BLOCKS):
+            for ig in range(I_GROUPS):
+                nc.sync.dma_start(out=w_words[:, jb, ig, :].bitcast(I32), in_=word_rows[ig, jb])
+
+        wl_sb = keep.tile([P, 2, 2 * FEATURES], BF16)
+        nc.sync.dma_start(out=wl_sb[:], in_=W_L.rearrange("(t o) k -> o t k", t=2))
+        bias_rows = keep.tile([P, 2 * WIDTH], BF16)
+        nc.vector.memset(bias_rows[:].bitcast(I32), 0)
+        nc.sync.dma_start(out=bias_rows[0:1, 0:WIDTH], in_=b_L.unsqueeze(0))
+        nc.sync.dma_start(out=bias_rows[0:1, WIDTH : 2 * WIDTH], in_=b_L2.unsqueeze(0))
+
+
+        hs_pairs = keep.tile([P, B_TILES, FEATURES, 2], BF16)
+        for half in range(HALVES):
+            tiles = slice(half * TILES_PER_HALF, (half + 1) * TILES_PER_HALF)
+            nc.vector.tensor_copy(
+                out=hs_pairs[:, tiles],
+                in_=hs_sb[:, tiles, :].unsqueeze(3).to_broadcast([P, TILES_PER_HALF, FEATURES, 2]),
+            )
+        hs_words = hs_pairs[:].rearrange("p n i e -> p n (i e)").bitcast(F32)
+        ht_words = ht_sb[:].bitcast(F32)
+
+        hs_rows = keep.tile([P, I_GROUPS, HALVES, HALF_B * 2], BF16)
+        ht_rows = keep.tile([P, J_BLOCKS, HALVES, HALF_B * PACK], BF16)
+
+        def make_hs_rows(ig, half):
+            tiles = slice(half * TILES_PER_HALF, (half + 1) * TILES_PER_HALF)
+            features = slice(ig * I_PER_PASS, (ig + 1) * I_PER_PASS)
+            hs_wide = spread.tile([P, TILES_PER_HALF, I_PER_PASS, BLOCK_P], F32)
+            nc.scalar.copy(
+                out=hs_wide[:],
+                in_=hs_words[:, tiles, features]
+                .unsqueeze(3)
+                .to_broadcast([P, TILES_PER_HALF, I_PER_PASS, BLOCK_P]),
+            )
+            bank = psum_work.tile([P, TILES_PER_HALF, P], F32, tag="work")
+            for n in range(TILES_PER_HALF):
+                nc.tensor.transpose(
+                    bank[:, n, :], hs_wide[:, n].rearrange("p s w -> p (s w)"), ident_f32[:]
+                )
+            nc.scalar.copy(
+                out=hs_rows[:, ig, half, :].bitcast(F32), in_=bank[:].rearrange("p n c -> p (n c)")
+            )
+
+        def make_ht_rows(jb, half):
+            tiles = slice(half * TILES_PER_HALF, (half + 1) * TILES_PER_HALF)
+            ht_wide = spread.tile([P, 2, TILES_PER_HALF, I_PER_PASS, BLOCK_P], F32)
+            for u in range(2):
+                words = slice(2 * BLOCK_P * jb + u, 2 * BLOCK_P * (jb + 1), 2)
+                nc.scalar.copy(
+                    out=ht_wide[:, u],
+                    in_=ht_words[:, tiles, words]
+                    .unsqueeze(2)
+                    .to_broadcast([P, TILES_PER_HALF, I_PER_PASS, BLOCK_P]),
+                )
+            for pair in range(TILES_PER_HALF // 2):
+                bank = psum_work.tile([P, 2, 2, P], F32, tag="work")
+                for n in range(2):
+                    for u in range(2):
+                        nc.tensor.transpose(
+                            bank[:, n, u, :],
+                            ht_wide[:, u, 2 * pair + n].rearrange("p s w -> p (s w)"),
+                            ident_f32[:],
+                        )
+                columns = slice(pair * 2 * P * PACK, (pair + 1) * 2 * P * PACK)
+                nc.scalar.copy(
+                    out=ht_rows[:, jb, half, columns]
+                    .bitcast(F32)
+                    .rearrange("p (n c u) -> p n c u", n=2, u=2),
+                    in_=bank[:].rearrange("p n u c -> p n c u"),
+                )
+
+        for half in range(HALVES):
+            make_ht_rows(0, half)
+            for ig in range(I_GROUPS):
+                make_hs_rows(ig, half)
+            for jb in range(1, J_BLOCKS):
+                make_ht_rows(jb, half)
+
+        out_sb = keep.tile([P, B_TILES, 2 * WIDTH], F32)
+        out_rows = out.rearrange("(c n) f -> c n f", n=B_TILES)
+
+        hsT = keep.tile([P, B_TILES, P], BF16)
+        htT = keep.tile([P, B_TILES, P], BF16)
+        for rows, turned in ((hs_sb, hsT), (ht_sb, htT)):
+            bank = psum_work.tile([P, B_TILES, P], BF16, tag="work")
+            for n in range(B_TILES):
+                nc.tensor.transpose(bank[:, n, :], rows[:, n, :], ident_bf16[:])
+            nc.scalar.copy(out=turned[:], in_=bank[:])
+        wlT = keep.tile([P, 2, WIDTH], BF16)
+        bank = psum_work.tile([P, 2, WIDTH], BF16, tag="work")
+        for kh in range(2):
+            for t in range(2):
+                nc.tensor.transpose(
+                    bank[:, kh, t * P : (t + 1) * P], wl_sb[:, t, kh * P : (kh + 1) * P], ident_bf16[:]
+                )
+        nc.scalar.copy(out=wlT[:], in_=bank[:])
+
+        bias_wide = keep.tile([P, WIDTH], F32)
+        bank = psum_work.tile([P, WIDTH], F32, tag="work")
+        nc.tensor.matmul(
+            bank[:], lhsT=ones[:], rhs=bias_rows[:, WIDTH : 2 * WIDTH], start=True, stop=True
+        )
+        nc.scalar.copy(out=bias_wide[:], in_=bank[:])
+
+        for pair in range(B_TILES // 2):
+            bank = psum_work.tile([P, 2, WIDTH], F32, tag="work")
+            for k in range(2):
+                n = 2 * pair + k
+                nc.tensor.matmul(bank[:, k, :], lhsT=hsT[:, n, :], rhs=wlT[:, 0, :], start=True, stop=False)
+                nc.tensor.matmul(bank[:, k, :], lhsT=htT[:, n, :], rhs=wlT[:, 1, :], start=False, stop=False)
+                nc.tensor.matmul(bank[:, k, :], lhsT=ones[:], rhs=bias_rows[:, 0:WIDTH], start=False, stop=True)
+            nc.scalar.copy(out=out_sb[:, 2 * pair : 2 * pair + 2, 0:WIDTH], in_=bank[:])
+            nc.sync.dma_start(
+                out=out_rows[:, 2 * pair : 2 * pair + 2, 0:WIDTH],
+                in_=out_sb[:, 2 * pair : 2 * pair + 2, 0:WIDTH],
+            )
+
+        product = None
+        acc = None
+        for step in range(STEPS + 1):
+            earlier = product
+            if step < STEPS:
+                half, jb, ig = place_of(step)
+                product = stream.tile([P, HALF_B * PACK], BF16, align_bytes=64)
+                nc.vector.tensor_tensor(
+                    out=product[:].rearrange("p (b u e) -> p b u e", u=2, e=2),
+                    in0=ht_rows[:, jb, half, :].rearrange("p (b u e) -> p b u e", u=2, e=2),
+                    in1=hs_rows[:, ig, half, :]
+                    .rearrange("p (b e) -> p b e", e=2)
+                    .unsqueeze(2)
+                    .to_broadcast([P, HALF_B, 2, 2]),
+                    op=mybir.AluOpType.mult,
+                )
+            if step > 0:
+                half, jb, ig = place_of(step - 1)
+                v_words = stream.tile([P, HALF_B], U32, align_bytes=64)
+                v_scales = stream.tile([P, HALF_B], U8, align_bytes=64)
+                nc.vector.quantize_mx(out=v_words[:].bitcast(FP8X4), scales=v_scales[:], in_=earlier[:])
+                first_pass = jb == 0 and ig == 0
+                last_pass = jb == J_BLOCKS - 1 and ig == I_GROUPS - 1
+                if first_pass:
+                    acc = [psum_acc.tile([P, WIDTH], F32, name="acc%d" % t) for t in range(TILES_PER_HALF)]
+                for t in range(TILES_PER_HALF):
+                    nc.tensor.matmul_mx(
+                        out=acc[t][:],
+                        lhsT=v_words[:, t * P : (t + 1) * P].bitcast(FP8X4),
+                        lhsT_scale=v_scales[:, t * P : (t + 1) * P],
+                        rhs=w_words[:, jb, ig, :].bitcast(FP8X4),
+                        rhs_scale=w_scales[:, ig, jb, :],
+                        start=first_pass,
+                        stop=last_pass,
+                    )
+                if last_pass:
+                    for t in range(TILES_PER_HALF):
+                        n = half * TILES_PER_HALF + t
+                        nc.vector.tensor_tensor(
+                            out=out_sb[:, n, WIDTH : 2 * WIDTH],
+                            in0=acc[t][:],
+                            in1=bias_wide[:],
+                            op=mybir.AluOpType.add,
+                        )
+                        nc.sync.dma_start(
+                            out=out_rows[:, n, WIDTH : 2 * WIDTH], in_=out_sb[:, n, WIDTH : 2 * WIDTH]
+                        )

@@ -23,15 +23,28 @@ B_TILES = BATCH // P
 HALVES = 2
 TILES_PER_HALF = B_TILES // HALVES
 HALF_B = TILES_PER_HALF * P
-STEPS = HALVES * J_BLOCKS * I_GROUPS
+
+SCALAR_GROUPS = 2
+VECTOR_GROUPS = I_GROUPS - SCALAR_GROUPS
+STEPS_PER_HALF = VECTOR_GROUPS * J_BLOCKS
+STEPS = HALVES * STEPS_PER_HALF
+UNITS_PER_HALF = SCALAR_GROUPS * TILES_PER_HALF
+STEPS_PER_UNIT = STEPS_PER_HALF // UNITS_PER_HALF
+assert STEPS_PER_UNIT * UNITS_PER_HALF == STEPS_PER_HALF
 
 FLOPS = 2 * BATCH * FEATURES * FEATURES * WIDTH + 2 * BATCH * 2 * FEATURES * WIDTH
 
 
-def place_of(step):
-    half, rest = divmod(step, J_BLOCKS * I_GROUPS)
-    jb, ig = divmod(rest, I_GROUPS)
-    return half, jb, ig
+def place_of_step(step):
+    half, rest = divmod(step, STEPS_PER_HALF)
+    ig, jb = divmod(rest, J_BLOCKS)
+    return half, ig, jb
+
+
+def place_of_unit(unit):
+    half, rest = divmod(unit, UNITS_PER_HALF)
+    group, t = divmod(rest, TILES_PER_HALF)
+    return half, VECTOR_GROUPS + group, t
 
 
 def tile_deepandwide_kernel(
@@ -41,7 +54,8 @@ def tile_deepandwide_kernel(
     with ExitStack() as ctx:
         keep = ctx.enter_context(tc.tile_pool(name="keep", bufs=1))
         spread = ctx.enter_context(tc.tile_pool(name="spread", bufs=2))
-        stream = ctx.enter_context(tc.tile_pool(name="stream", bufs=3))
+        units = ctx.enter_context(tc.tile_pool(name="units", bufs=2))
+        stream = ctx.enter_context(tc.tile_pool(name="stream", bufs=4))
         psum_acc = ctx.enter_context(tc.psum_pool(name="psum_acc", bufs=1))
         psum_work = ctx.enter_context(tc.psum_pool(name="psum_work", bufs=4))
 
@@ -70,15 +84,20 @@ def tile_deepandwide_kernel(
                 in_=scale_rows[Q],
             )
 
-        w_words = keep.tile([P, J_BLOCKS, I_GROUPS, WIDTH], U32, align_bytes=64)
+        w_words = keep.tile([P, I_GROUPS, J_BLOCKS, WIDTH], U32, align_bytes=64)
         word_rows = (
             W_L2_words.rearrange("g p n t -> (g p) (n t)")
             .bitcast(I32)
             .rearrange("(ig s jb w) x -> ig jb s w x", ig=I_GROUPS, s=I_PER_PASS, jb=J_BLOCKS, w=BLOCK_P)
         )
-        for jb in range(J_BLOCKS):
-            for ig in range(I_GROUPS):
-                nc.sync.dma_start(out=w_words[:, jb, ig, :].bitcast(I32), in_=word_rows[ig, jb])
+        load_order = []
+        for group in range(VECTOR_GROUPS):
+            load_order.append(group)
+            if group < SCALAR_GROUPS:
+                load_order.append(VECTOR_GROUPS + group)
+        for ig in load_order:
+            for jb in range(J_BLOCKS):
+                nc.sync.dma_start(out=w_words[:, ig, jb, :].bitcast(I32), in_=word_rows[ig, jb])
 
         wl_sb = keep.tile([P, 2, 2 * FEATURES], BF16)
         nc.sync.dma_start(out=wl_sb[:], in_=W_L.rearrange("(t o) k -> o t k", t=2))
@@ -98,14 +117,14 @@ def tile_deepandwide_kernel(
         hs_words = hs_pairs[:].rearrange("p n i e -> p n (i e)").bitcast(F32)
         ht_words = ht_sb[:].bitcast(F32)
 
-        hs_rows = keep.tile([P, I_GROUPS, HALVES, HALF_B * 2], BF16)
+        hs_rows = keep.tile([P, VECTOR_GROUPS, HALVES, HALF_B * 2], BF16)
         ht_rows = keep.tile([P, J_BLOCKS, HALVES, HALF_B * PACK], BF16)
 
-        def make_hs_rows(ig, half):
+        def make_hs_rows(ig, half, repeat):
             tiles = slice(half * TILES_PER_HALF, (half + 1) * TILES_PER_HALF)
             features = slice(ig * I_PER_PASS, (ig + 1) * I_PER_PASS)
             hs_wide = spread.tile([P, TILES_PER_HALF, I_PER_PASS, BLOCK_P], F32)
-            nc.scalar.copy(
+            repeat(
                 out=hs_wide[:],
                 in_=hs_words[:, tiles, features]
                 .unsqueeze(3)
@@ -120,12 +139,12 @@ def tile_deepandwide_kernel(
                 out=hs_rows[:, ig, half, :].bitcast(F32), in_=bank[:].rearrange("p n c -> p (n c)")
             )
 
-        def make_ht_rows(jb, half):
+        def make_ht_rows(jb, half, repeat):
             tiles = slice(half * TILES_PER_HALF, (half + 1) * TILES_PER_HALF)
             ht_wide = spread.tile([P, 2, TILES_PER_HALF, I_PER_PASS, BLOCK_P], F32)
             for u in range(2):
                 words = slice(2 * BLOCK_P * jb + u, 2 * BLOCK_P * (jb + 1), 2)
-                nc.scalar.copy(
+                repeat(
                     out=ht_wide[:, u],
                     in_=ht_words[:, tiles, words]
                     .unsqueeze(2)
@@ -148,40 +167,79 @@ def tile_deepandwide_kernel(
                     in_=bank[:].rearrange("p n u c -> p n c u"),
                 )
 
-        for half in range(HALVES):
-            make_ht_rows(0, half)
-            for ig in range(I_GROUPS):
-                make_hs_rows(ig, half)
-            for jb in range(1, J_BLOCKS):
-                make_ht_rows(jb, half)
+        make_ht_rows(0, 0, nc.vector.tensor_copy)
+        make_hs_rows(0, 0, nc.vector.tensor_copy)
+        for jb in range(1, J_BLOCKS):
+            make_ht_rows(jb, 0, nc.vector.tensor_copy)
+
+        ht_sorted = keep.tile([P, B_TILES, 2 * J_BLOCKS, 2 * BLOCK_P], BF16)
+        nc.vector.tensor_copy(
+            out=ht_sorted[:]
+            .rearrange("p n a x -> p (n a x)")
+            .bitcast(F32)
+            .rearrange("p (m u w) -> p m u w", u=2, w=BLOCK_P),
+            in_=ht_words.rearrange("p n (jb w u) -> p (n jb) u w", w=BLOCK_P, u=2),
+        )
+        hs_f32 = keep.tile([P, B_TILES, SCALAR_GROUPS * I_PER_PASS], F32)
+        nc.vector.tensor_copy(out=hs_f32[:], in_=hs_sb[:, :, VECTOR_GROUPS * I_PER_PASS :])
+
+        def multiply_unit(half, ig, t):
+            n = half * TILES_PER_HALF + t
+            by_batch = units.tile([P, 2 * J_BLOCKS, I_PER_PASS, 2 * BLOCK_P], BF16)
+            for s in range(I_PER_PASS):
+                column = (ig - VECTOR_GROUPS) * I_PER_PASS + s
+                nc.scalar.activation(
+                    out=by_batch[:, :, s, :],
+                    in_=ht_sorted[:, n],
+                    func=mybir.ActivationFunctionType.Copy,
+                    scale=hs_f32[:, n, column : column + 1],
+                )
+            unit_product = units.tile([P, J_BLOCKS * P * PACK], BF16, align_bytes=64)
+            for pair in range(J_BLOCKS // 2):
+                bank = psum_work.tile([P, 2, 2, P], F32, tag="work")
+                for j in range(2):
+                    for u in range(2):
+                        nc.tensor.transpose(
+                            bank[:, j, u, :],
+                            by_batch[:, 4 * pair + 2 * j + u].rearrange("p s x -> p (s x)").bitcast(F32),
+                            ident_f32[:],
+                        )
+                columns = slice(pair * 2 * P * PACK, (pair + 1) * 2 * P * PACK)
+                nc.scalar.copy(
+                    out=unit_product[:, columns]
+                    .bitcast(F32)
+                    .rearrange("p (j c u) -> p j c u", j=2, u=2),
+                    in_=bank[:].rearrange("p j u c -> p j c u"),
+                )
+            return unit_product
 
         out_sb = keep.tile([P, B_TILES, 2 * WIDTH], F32)
         out_rows = out.rearrange("(c n) f -> c n f", n=B_TILES)
-
         hsT = keep.tile([P, B_TILES, P], BF16)
         htT = keep.tile([P, B_TILES, P], BF16)
-        for rows, turned in ((hs_sb, hsT), (ht_sb, htT)):
-            bank = psum_work.tile([P, B_TILES, P], BF16, tag="work")
-            for n in range(B_TILES):
-                nc.tensor.transpose(bank[:, n, :], rows[:, n, :], ident_bf16[:])
-            nc.scalar.copy(out=turned[:], in_=bank[:])
         wlT = keep.tile([P, 2, WIDTH], BF16)
-        bank = psum_work.tile([P, 2, WIDTH], BF16, tag="work")
-        for kh in range(2):
-            for t in range(2):
-                nc.tensor.transpose(
-                    bank[:, kh, t * P : (t + 1) * P], wl_sb[:, t, kh * P : (kh + 1) * P], ident_bf16[:]
-                )
-        nc.scalar.copy(out=wlT[:], in_=bank[:])
-
         bias_wide = keep.tile([P, WIDTH], F32)
-        bank = psum_work.tile([P, WIDTH], F32, tag="work")
-        nc.tensor.matmul(
-            bank[:], lhsT=ones[:], rhs=bias_rows[:, WIDTH : 2 * WIDTH], start=True, stop=True
-        )
-        nc.scalar.copy(out=bias_wide[:], in_=bank[:])
 
-        for pair in range(B_TILES // 2):
+        def prepare_deep_path():
+            for rows, turned in ((hs_sb, hsT), (ht_sb, htT)):
+                bank = psum_work.tile([P, B_TILES, P], BF16, tag="work")
+                for n in range(B_TILES):
+                    nc.tensor.transpose(bank[:, n, :], rows[:, n, :], ident_bf16[:])
+                nc.scalar.copy(out=turned[:], in_=bank[:])
+            bank = psum_work.tile([P, 2, WIDTH], BF16, tag="work")
+            for kh in range(2):
+                for t in range(2):
+                    nc.tensor.transpose(
+                        bank[:, kh, t * P : (t + 1) * P], wl_sb[:, t, kh * P : (kh + 1) * P], ident_bf16[:]
+                    )
+            nc.scalar.copy(out=wlT[:], in_=bank[:])
+            bank = psum_work.tile([P, WIDTH], F32, tag="work")
+            nc.tensor.matmul(
+                bank[:], lhsT=ones[:], rhs=bias_rows[:, WIDTH : 2 * WIDTH], start=True, stop=True
+            )
+            nc.scalar.copy(out=bias_wide[:], in_=bank[:])
+
+        def deep_path(pair):
             bank = psum_work.tile([P, 2, WIDTH], F32, tag="work")
             for k in range(2):
                 n = 2 * pair + k
@@ -194,12 +252,45 @@ def tile_deepandwide_kernel(
                 in_=out_sb[:, 2 * pair : 2 * pair + 2, 0:WIDTH],
             )
 
+        def quantise(operand):
+            v_words = stream.tile([P, HALF_B], U32, align_bytes=64)
+            v_scales = stream.tile([P, HALF_B], U8, align_bytes=64)
+            nc.vector.quantize_mx(out=v_words[:].bitcast(FP8X4), scales=v_scales[:], in_=operand[:])
+            return v_words, v_scales
+
+        def contract(total, v_words, v_scales, piece, ig, jb, start, stop):
+            columns = slice(piece * P, (piece + 1) * P)
+            nc.tensor.matmul_mx(
+                out=total[:],
+                lhsT=v_words[:, columns].bitcast(FP8X4),
+                lhsT_scale=v_scales[:, columns],
+                rhs=w_words[:, ig, jb, :].bitcast(FP8X4),
+                rhs_scale=w_scales[:, ig, jb, :],
+                start=start,
+                stop=stop,
+            )
+
         product = None
+        unit_product = None
         acc = None
         for step in range(STEPS + 1):
             earlier = product
+            earlier_unit = unit_product
             if step < STEPS:
-                half, jb, ig = place_of(step)
+                half, ig, jb = place_of_step(step)
+                if step % STEPS_PER_UNIT == 0:
+                    unit_product = multiply_unit(*place_of_unit(step // STEPS_PER_UNIT))
+                group = half * VECTOR_GROUPS + ig
+                if jb == 0 and group + 1 < HALVES * VECTOR_GROUPS:
+                    next_half, next_ig = divmod(group + 1, VECTOR_GROUPS)
+                    make_hs_rows(next_ig, next_half, nc.scalar.copy)
+                if jb == 2:
+                    if group < J_BLOCKS:
+                        make_ht_rows(group, 1, nc.scalar.copy)
+                    elif group == J_BLOCKS:
+                        prepare_deep_path()
+                    elif group <= J_BLOCKS + B_TILES // 2:
+                        deep_path(group - J_BLOCKS - 1)
                 product = stream.tile([P, HALF_B * PACK], BF16, align_bytes=64)
                 nc.vector.tensor_tensor(
                     out=product[:].rearrange("p (b u e) -> p b u e", u=2, e=2),
@@ -211,24 +302,19 @@ def tile_deepandwide_kernel(
                     op=mybir.AluOpType.mult,
                 )
             if step > 0:
-                half, jb, ig = place_of(step - 1)
-                v_words = stream.tile([P, HALF_B], U32, align_bytes=64)
-                v_scales = stream.tile([P, HALF_B], U8, align_bytes=64)
-                nc.vector.quantize_mx(out=v_words[:].bitcast(FP8X4), scales=v_scales[:], in_=earlier[:])
-                first_pass = jb == 0 and ig == 0
-                last_pass = jb == J_BLOCKS - 1 and ig == I_GROUPS - 1
+                if step % STEPS_PER_UNIT == 0:
+                    half, ig, t = place_of_unit(step // STEPS_PER_UNIT - 1)
+                    v_words, v_scales = quantise(earlier_unit)
+                    for jb in range(J_BLOCKS):
+                        contract(acc[t], v_words, v_scales, jb, ig, jb, False, False)
+                half, ig, jb = place_of_step(step - 1)
+                v_words, v_scales = quantise(earlier)
+                first_pass = ig == 0 and jb == 0
+                last_pass = ig == VECTOR_GROUPS - 1 and jb == J_BLOCKS - 1
                 if first_pass:
                     acc = [psum_acc.tile([P, WIDTH], F32, name="acc%d" % t) for t in range(TILES_PER_HALF)]
                 for t in range(TILES_PER_HALF):
-                    nc.tensor.matmul_mx(
-                        out=acc[t][:],
-                        lhsT=v_words[:, t * P : (t + 1) * P].bitcast(FP8X4),
-                        lhsT_scale=v_scales[:, t * P : (t + 1) * P],
-                        rhs=w_words[:, jb, ig, :].bitcast(FP8X4),
-                        rhs_scale=w_scales[:, ig, jb, :],
-                        start=first_pass,
-                        stop=last_pass,
-                    )
+                    contract(acc[t], v_words, v_scales, t, ig, jb, first_pass, last_pass)
                 if last_pass:
                     for t in range(TILES_PER_HALF):
                         n = half * TILES_PER_HALF + t

@@ -24,27 +24,17 @@ HALVES = 2
 TILES_PER_HALF = B_TILES // HALVES
 HALF_B = TILES_PER_HALF * P
 
-SCALAR_GROUPS = 2
-VECTOR_GROUPS = I_GROUPS - SCALAR_GROUPS
-STEPS_PER_HALF = VECTOR_GROUPS * J_BLOCKS
-STEPS = HALVES * STEPS_PER_HALF
-UNITS_PER_HALF = SCALAR_GROUPS * TILES_PER_HALF
-STEPS_PER_UNIT = STEPS_PER_HALF // UNITS_PER_HALF
-assert STEPS_PER_UNIT * UNITS_PER_HALF == STEPS_PER_HALF
+SCALAR_GROUPS = (1, 2)
+FIRST_SCALAR_GROUP = I_GROUPS - max(SCALAR_GROUPS)
+STEPS_PER_UNIT = tuple(
+    (I_GROUPS - groups) * J_BLOCKS // (groups * TILES_PER_HALF) for groups in SCALAR_GROUPS
+)
+assert all(
+    STEPS_PER_UNIT[h] * SCALAR_GROUPS[h] * TILES_PER_HALF == (I_GROUPS - SCALAR_GROUPS[h]) * J_BLOCKS
+    for h in range(HALVES)
+)
 
 FLOPS = 2 * BATCH * FEATURES * FEATURES * WIDTH + 2 * BATCH * 2 * FEATURES * WIDTH
-
-
-def place_of_step(step):
-    half, rest = divmod(step, STEPS_PER_HALF)
-    ig, jb = divmod(rest, J_BLOCKS)
-    return half, ig, jb
-
-
-def place_of_unit(unit):
-    half, rest = divmod(unit, UNITS_PER_HALF)
-    group, t = divmod(rest, TILES_PER_HALF)
-    return half, VECTOR_GROUPS + group, t
 
 
 def tile_deepandwide_kernel(
@@ -90,12 +80,7 @@ def tile_deepandwide_kernel(
             .bitcast(I32)
             .rearrange("(ig s jb w) x -> ig jb s w x", ig=I_GROUPS, s=I_PER_PASS, jb=J_BLOCKS, w=BLOCK_P)
         )
-        load_order = []
-        for group in range(VECTOR_GROUPS):
-            load_order.append(group)
-            if group < SCALAR_GROUPS:
-                load_order.append(VECTOR_GROUPS + group)
-        for ig in load_order:
+        for ig in range(I_GROUPS):
             for jb in range(J_BLOCKS):
                 nc.sync.dma_start(out=w_words[:, ig, jb, :].bitcast(I32), in_=word_rows[ig, jb])
 
@@ -117,7 +102,7 @@ def tile_deepandwide_kernel(
         hs_words = hs_pairs[:].rearrange("p n i e -> p n (i e)").bitcast(F32)
         ht_words = ht_sb[:].bitcast(F32)
 
-        hs_rows = keep.tile([P, VECTOR_GROUPS, HALVES, HALF_B * 2], BF16)
+        hs_rows = keep.tile([P, I_GROUPS - min(SCALAR_GROUPS), HALVES, HALF_B * 2], BF16)
         ht_rows = keep.tile([P, J_BLOCKS, HALVES, HALF_B * PACK], BF16)
 
         def make_hs_rows(ig, half, repeat):
@@ -180,14 +165,14 @@ def tile_deepandwide_kernel(
             .rearrange("p (m u w) -> p m u w", u=2, w=BLOCK_P),
             in_=ht_words.rearrange("p n (jb w u) -> p (n jb) u w", w=BLOCK_P, u=2),
         )
-        hs_f32 = keep.tile([P, B_TILES, SCALAR_GROUPS * I_PER_PASS], F32)
-        nc.vector.tensor_copy(out=hs_f32[:], in_=hs_sb[:, :, VECTOR_GROUPS * I_PER_PASS :])
+        hs_f32 = keep.tile([P, B_TILES, max(SCALAR_GROUPS) * I_PER_PASS], F32)
+        nc.vector.tensor_copy(out=hs_f32[:], in_=hs_sb[:, :, FIRST_SCALAR_GROUP * I_PER_PASS :])
 
         def multiply_unit(half, ig, t):
             n = half * TILES_PER_HALF + t
             by_batch = units.tile([P, 2 * J_BLOCKS, I_PER_PASS, 2 * BLOCK_P], BF16)
             for s in range(I_PER_PASS):
-                column = (ig - VECTOR_GROUPS) * I_PER_PASS + s
+                column = (ig - FIRST_SCALAR_GROUP) * I_PER_PASS + s
                 nc.scalar.activation(
                     out=by_batch[:, :, s, :],
                     in_=ht_sorted[:, n],
@@ -270,60 +255,79 @@ def tile_deepandwide_kernel(
                 stop=stop,
             )
 
-        product = None
-        unit_product = None
-        acc = None
-        for step in range(STEPS + 1):
-            earlier = product
-            earlier_unit = unit_product
-            if step < STEPS:
-                half, ig, jb = place_of_step(step)
-                if step % STEPS_PER_UNIT == 0:
-                    unit_product = multiply_unit(*place_of_unit(step // STEPS_PER_UNIT))
-                group = half * VECTOR_GROUPS + ig
-                if jb == 0 and group + 1 < HALVES * VECTOR_GROUPS:
-                    next_half, next_ig = divmod(group + 1, VECTOR_GROUPS)
-                    make_hs_rows(next_ig, next_half, nc.scalar.copy)
-                if jb == 2:
-                    if group < J_BLOCKS:
-                        make_ht_rows(group, 1, nc.scalar.copy)
-                    elif group == J_BLOCKS:
-                        prepare_deep_path()
-                    elif group <= J_BLOCKS + B_TILES // 2:
-                        deep_path(group - J_BLOCKS - 1)
-                product = stream.tile([P, HALF_B * PACK], BF16, align_bytes=64)
-                nc.vector.tensor_tensor(
-                    out=product[:].rearrange("p (b u e) -> p b u e", u=2, e=2),
-                    in0=ht_rows[:, jb, half, :].rearrange("p (b u e) -> p b u e", u=2, e=2),
-                    in1=hs_rows[:, ig, half, :]
-                    .rearrange("p (b e) -> p b e", e=2)
-                    .unsqueeze(2)
-                    .to_broadcast([P, HALF_B, 2, 2]),
-                    op=mybir.AluOpType.mult,
-                )
-            if step > 0:
-                if step % STEPS_PER_UNIT == 0:
-                    half, ig, t = place_of_unit(step // STEPS_PER_UNIT - 1)
-                    v_words, v_scales = quantise(earlier_unit)
-                    for jb in range(J_BLOCKS):
-                        contract(acc[t], v_words, v_scales, jb, ig, jb, False, False)
-                half, ig, jb = place_of_step(step - 1)
-                v_words, v_scales = quantise(earlier)
-                first_pass = ig == 0 and jb == 0
-                last_pass = ig == VECTOR_GROUPS - 1 and jb == J_BLOCKS - 1
+        def multiply_step(half, ig, jb):
+            product = stream.tile([P, HALF_B * PACK], BF16, align_bytes=64)
+            nc.vector.tensor_tensor(
+                out=product[:].rearrange("p (b u e) -> p b u e", u=2, e=2),
+                in0=ht_rows[:, jb, half, :].rearrange("p (b u e) -> p b u e", u=2, e=2),
+                in1=hs_rows[:, ig, half, :]
+                .rearrange("p (b e) -> p b e", e=2)
+                .unsqueeze(2)
+                .to_broadcast([P, HALF_B, 2, 2]),
+                op=mybir.AluOpType.mult,
+            )
+            return product
+
+        acc = {}
+
+        def contract_unit(unit_product, half, ig, t):
+            v_words, v_scales = quantise(unit_product)
+            for jb in range(J_BLOCKS):
+                contract(acc[(half, t)], v_words, v_scales, jb, ig, jb, False, False)
+
+        def contract_step(product, half, ig, jb):
+            v_words, v_scales = quantise(product)
+            first_pass = ig == 0 and jb == 0
+            last_pass = ig == I_GROUPS - SCALAR_GROUPS[half] - 1 and jb == J_BLOCKS - 1
+            for t in range(TILES_PER_HALF):
                 if first_pass:
-                    acc = [psum_acc.tile([P, WIDTH], F32, name="acc%d" % t) for t in range(TILES_PER_HALF)]
+                    acc[(half, t)] = psum_acc.tile([P, WIDTH], F32, name="acc%d" % t)
+                contract(acc[(half, t)], v_words, v_scales, t, ig, jb, first_pass, last_pass)
+            if last_pass:
                 for t in range(TILES_PER_HALF):
-                    contract(acc[t], v_words, v_scales, t, ig, jb, first_pass, last_pass)
-                if last_pass:
-                    for t in range(TILES_PER_HALF):
-                        n = half * TILES_PER_HALF + t
-                        nc.vector.tensor_tensor(
-                            out=out_sb[:, n, WIDTH : 2 * WIDTH],
-                            in0=acc[t][:],
-                            in1=bias_wide[:],
-                            op=mybir.AluOpType.add,
-                        )
-                        nc.sync.dma_start(
-                            out=out_rows[:, n, WIDTH : 2 * WIDTH], in_=out_sb[:, n, WIDTH : 2 * WIDTH]
-                        )
+                    n = half * TILES_PER_HALF + t
+                    nc.vector.tensor_tensor(
+                        out=out_sb[:, n, WIDTH : 2 * WIDTH],
+                        in0=acc[(half, t)][:],
+                        in1=bias_wide[:],
+                        op=mybir.AluOpType.add,
+                    )
+                    nc.sync.dma_start(
+                        out=out_rows[:, n, WIDTH : 2 * WIDTH], in_=out_sb[:, n, WIDTH : 2 * WIDTH]
+                    )
+
+        later = [lambda jb=jb: make_ht_rows(jb, 1, nc.scalar.copy) for jb in range(J_BLOCKS)]
+        later.append(prepare_deep_path)
+        later.extend([lambda pair=pair: deep_path(pair) for pair in range(B_TILES // 2)])
+        pieces_done = 0
+
+        waiting_step = None
+        waiting_unit = None
+        for half in range(HALVES):
+            vector_groups = I_GROUPS - SCALAR_GROUPS[half]
+            for ig in range(vector_groups):
+                for jb in range(J_BLOCKS):
+                    step = ig * J_BLOCKS + jb
+                    if jb == 0:
+                        if ig + 1 < vector_groups:
+                            make_hs_rows(ig + 1, half, nc.scalar.copy)
+                        elif half + 1 < HALVES:
+                            make_hs_rows(0, half + 1, nc.scalar.copy)
+                    started_unit = None
+                    if step % STEPS_PER_UNIT[half] == 0:
+                        group, t = divmod(step // STEPS_PER_UNIT[half], TILES_PER_HALF)
+                        unit_ig = vector_groups + group
+                        started_unit = (multiply_unit(half, unit_ig, t), half, unit_ig, t)
+                    if jb % 2 == 1 and pieces_done < len(later):
+                        later[pieces_done]()
+                        pieces_done += 1
+                    product = multiply_step(half, ig, jb)
+                    if started_unit is not None:
+                        if waiting_unit is not None:
+                            contract_unit(*waiting_unit)
+                        waiting_unit = started_unit
+                    if waiting_step is not None:
+                        contract_step(*waiting_step)
+                    waiting_step = (product, half, ig, jb)
+        contract_unit(*waiting_unit)
+        contract_step(*waiting_step)

@@ -24,17 +24,24 @@ HALVES = 2
 TILES_PER_HALF = B_TILES // HALVES
 HALF_B = TILES_PER_HALF * P
 
-SCALAR_GROUPS = (1, 2)
-FIRST_SCALAR_GROUP = I_GROUPS - max(SCALAR_GROUPS)
-STEPS_PER_UNIT = tuple(
-    (I_GROUPS - groups) * J_BLOCKS // (groups * TILES_PER_HALF) for groups in SCALAR_GROUPS
-)
-assert all(
-    STEPS_PER_UNIT[h] * SCALAR_GROUPS[h] * TILES_PER_HALF == (I_GROUPS - SCALAR_GROUPS[h]) * J_BLOCKS
-    for h in range(HALVES)
-)
+SCALAR_GROUPS = 2
+VECTOR_GROUPS = I_GROUPS - SCALAR_GROUPS
+STEPS_PER_UNIT = VECTOR_GROUPS * J_BLOCKS // (SCALAR_GROUPS * TILES_PER_HALF)
+assert STEPS_PER_UNIT * SCALAR_GROUPS * TILES_PER_HALF == VECTOR_GROUPS * J_BLOCKS
+STEPS_PER_HALF = J_BLOCKS * VECTOR_GROUPS
+STEPS = HALVES * STEPS_PER_HALF
+HT_AHEAD = VECTOR_GROUPS
+HST_AHEAD = VECTOR_GROUPS + 2
+HS_AHEAD = 2
+UNIT_LAG = 2
 
 FLOPS = 2 * BATCH * FEATURES * FEATURES * WIDTH + 2 * BATCH * 2 * FEATURES * WIDTH
+
+
+def place_of(step):
+    half, rest = divmod(step, STEPS_PER_HALF)
+    jb, ig = divmod(rest, VECTOR_GROUPS)
+    return half, jb, ig
 
 
 def tile_deepandwide_kernel(
@@ -44,22 +51,22 @@ def tile_deepandwide_kernel(
     with ExitStack() as ctx:
         keep = ctx.enter_context(tc.tile_pool(name="keep", bufs=1))
         spread = ctx.enter_context(tc.tile_pool(name="spread", bufs=2))
-        units = ctx.enter_context(tc.tile_pool(name="units", bufs=2))
-        stream = ctx.enter_context(tc.tile_pool(name="stream", bufs=4))
+        units = ctx.enter_context(tc.tile_pool(name="units", bufs=UNIT_LAG + 1))
+        stream = ctx.enter_context(tc.tile_pool(name="stream", bufs=6))
         psum_acc = ctx.enter_context(tc.psum_pool(name="psum_acc", bufs=1))
         psum_work = ctx.enter_context(tc.psum_pool(name="psum_work", bufs=4))
 
-        ident_f32 = keep.tile([P, P], F32)
-        make_identity(nc, ident_f32[:])
         ident_bf16 = keep.tile([P, P], BF16)
         make_identity(nc, ident_bf16[:])
+        ident_f32 = keep.tile([P, P], F32)
+        make_identity(nc, ident_f32[:])
         ones = keep.tile([P, P], BF16)
         nc.gpsimd.memset(ones[:], 1.0)
 
-        ht_sb = keep.tile([P, B_TILES, FEATURES], BF16)
-        nc.sync.dma_start(out=ht_sb[:], in_=htext.rearrange("(c n) j -> c n j", n=B_TILES))
         hs_sb = keep.tile([P, B_TILES, FEATURES], BF16)
         nc.sync.dma_start(out=hs_sb[:], in_=hspatial.rearrange("(c n) i -> c n i", n=B_TILES))
+        ht_sb = keep.tile([P, B_TILES, FEATURES], BF16)
+        nc.sync.dma_start(out=ht_sb[:], in_=htext.rearrange("(c n) j -> c n j", n=B_TILES))
 
         w_scales = keep.tile([P, I_GROUPS, J_BLOCKS, WIDTH], U8, align_bytes=64)
         nc.vector.memset(w_scales[:].rearrange("p a b n -> p (a b n)").bitcast(I32), 0)
@@ -80,9 +87,13 @@ def tile_deepandwide_kernel(
             .bitcast(I32)
             .rearrange("(ig s jb w) x -> ig jb s w x", ig=I_GROUPS, s=I_PER_PASS, jb=J_BLOCKS, w=BLOCK_P)
         )
-        for ig in range(I_GROUPS):
-            for jb in range(J_BLOCKS):
-                nc.sync.dma_start(out=w_words[:, ig, jb, :].bitcast(I32), in_=word_rows[ig, jb])
+        load_order = []
+        for jb in range(J_BLOCKS):
+            load_order.extend([(ig, jb) for ig in range(VECTOR_GROUPS)])
+            if jb < SCALAR_GROUPS:
+                load_order.extend([(VECTOR_GROUPS + jb, other) for other in range(J_BLOCKS)])
+        for ig, jb in load_order:
+            nc.sync.dma_start(out=w_words[:, ig, jb, :].bitcast(I32), in_=word_rows[ig, jb])
 
         wl_sb = keep.tile([P, 2, 2 * FEATURES], BF16)
         nc.sync.dma_start(out=wl_sb[:], in_=W_L.rearrange("(t o) k -> o t k", t=2))
@@ -91,45 +102,45 @@ def tile_deepandwide_kernel(
         nc.sync.dma_start(out=bias_rows[0:1, 0:WIDTH], in_=b_L.unsqueeze(0))
         nc.sync.dma_start(out=bias_rows[0:1, WIDTH : 2 * WIDTH], in_=b_L2.unsqueeze(0))
 
-
-        hs_pairs = keep.tile([P, B_TILES, FEATURES, 2], BF16)
-        for half in range(HALVES):
-            tiles = slice(half * TILES_PER_HALF, (half + 1) * TILES_PER_HALF)
-            nc.vector.tensor_copy(
-                out=hs_pairs[:, tiles],
-                in_=hs_sb[:, tiles, :].unsqueeze(3).to_broadcast([P, TILES_PER_HALF, FEATURES, 2]),
-            )
-        hs_words = hs_pairs[:].rearrange("p n i e -> p n (i e)").bitcast(F32)
-        ht_words = ht_sb[:].bitcast(F32)
-
-        hs_rows = keep.tile([P, I_GROUPS - min(SCALAR_GROUPS), HALVES, HALF_B * 2], BF16)
+        hs_rows = keep.tile([P, VECTOR_GROUPS, HALVES, HALF_B * 2], BF16)
         ht_rows = keep.tile([P, J_BLOCKS, HALVES, HALF_B * PACK], BF16)
 
-        def make_hs_rows(ig, half, repeat):
-            tiles = slice(half * TILES_PER_HALF, (half + 1) * TILES_PER_HALF)
-            features = slice(ig * I_PER_PASS, (ig + 1) * I_PER_PASS)
-            hs_wide = spread.tile([P, TILES_PER_HALF, I_PER_PASS, BLOCK_P], F32)
-            repeat(
-                out=hs_wide[:],
-                in_=hs_words[:, tiles, features]
-                .unsqueeze(3)
-                .to_broadcast([P, TILES_PER_HALF, I_PER_PASS, BLOCK_P]),
-            )
-            bank = psum_work.tile([P, TILES_PER_HALF, P], F32, tag="work")
-            for n in range(TILES_PER_HALF):
-                nc.tensor.transpose(
-                    bank[:, n, :], hs_wide[:, n].rearrange("p s w -> p (s w)"), ident_f32[:]
-                )
-            nc.scalar.copy(
-                out=hs_rows[:, ig, half, :].bitcast(F32), in_=bank[:].rearrange("p n c -> p (n c)")
-            )
 
-        def make_ht_rows(jb, half, repeat):
+        hsT = keep.tile([P, B_TILES, P], BF16)
+
+        def make_hsT(half):
+            tiles = slice(half * TILES_PER_HALF, (half + 1) * TILES_PER_HALF)
+            bank = psum_work.tile([P, TILES_PER_HALF, P], BF16, tag="work")
+            for t in range(TILES_PER_HALF):
+                nc.tensor.transpose(bank[:, t, :], hs_sb[:, half * TILES_PER_HALF + t, :], ident_bf16[:])
+            nc.scalar.copy(out=hsT[:, tiles], in_=bank[:])
+
+        choose = keep.tile([P, FEATURES, BLOCK_P], BF16)
+        nc.vector.tensor_copy(
+            out=choose[:], in_=ident_bf16[:].unsqueeze(2).to_broadcast([P, FEATURES, BLOCK_P])
+        )
+
+        def make_hs_rows(ig, half, copy):
+            bank = psum_work.tile([P, 2, 2, P, 2], BF16, tag="work")
+            for k in range(2):
+                first = half * TILES_PER_HALF + 2 * k
+                nc.tensor.matmul(
+                    bank[:, k],
+                    lhsT=choose[:, ig * I_PER_PASS : (ig + 1) * I_PER_PASS, :].rearrange("p s w -> p (s w)"),
+                    rhs=hsT[:, first : first + 2, :].unsqueeze(3).to_broadcast([P, 2, P, 2]),
+                    start=True,
+                    stop=True,
+                )
+            copy(out=hs_rows[:, ig, half, :], in_=bank[:].rearrange("p k n c e -> p (k n c e)"))
+
+        ht_words = ht_sb[:].bitcast(F32)
+
+        def make_ht_rows(jb, half, copy):
             tiles = slice(half * TILES_PER_HALF, (half + 1) * TILES_PER_HALF)
             ht_wide = spread.tile([P, 2, TILES_PER_HALF, I_PER_PASS, BLOCK_P], F32)
             for u in range(2):
                 words = slice(2 * BLOCK_P * jb + u, 2 * BLOCK_P * (jb + 1), 2)
-                repeat(
+                copy(
                     out=ht_wide[:, u],
                     in_=ht_words[:, tiles, words]
                     .unsqueeze(2)
@@ -145,17 +156,32 @@ def tile_deepandwide_kernel(
                             ident_f32[:],
                         )
                 columns = slice(pair * 2 * P * PACK, (pair + 1) * 2 * P * PACK)
-                nc.scalar.copy(
+                copy(
                     out=ht_rows[:, jb, half, columns]
                     .bitcast(F32)
                     .rearrange("p (n c u) -> p n c u", n=2, u=2),
                     in_=bank[:].rearrange("p n u c -> p n c u"),
                 )
 
-        make_ht_rows(0, 0, nc.vector.tensor_copy)
-        make_hs_rows(0, 0, nc.vector.tensor_copy)
-        for jb in range(1, J_BLOCKS):
-            make_ht_rows(jb, 0, nc.vector.tensor_copy)
+        def build_ahead(step):
+            first_use = step + HS_AHEAD
+            if 0 <= first_use < STEPS:
+                half, jb, ig = place_of(first_use)
+                if jb == 0:
+                    make_hs_rows(ig, half, nc.vector.tensor_copy if first_use == 0 else nc.scalar.copy)
+            first_use = step + HT_AHEAD
+            if 0 <= first_use < STEPS:
+                half, jb, ig = place_of(first_use)
+                if ig == 0:
+                    make_ht_rows(jb, half, nc.vector.tensor_copy if first_use == 0 else nc.scalar.copy)
+            first_use = step + HST_AHEAD
+            if 0 <= first_use < STEPS:
+                half, jb, ig = place_of(first_use)
+                if jb == 0 and ig == 0:
+                    make_hsT(half)
+
+        for step in range(-HST_AHEAD, 0):
+            build_ahead(step)
 
         ht_sorted = keep.tile([P, B_TILES, 2 * J_BLOCKS, 2 * BLOCK_P], BF16)
         nc.vector.tensor_copy(
@@ -165,14 +191,14 @@ def tile_deepandwide_kernel(
             .rearrange("p (m u w) -> p m u w", u=2, w=BLOCK_P),
             in_=ht_words.rearrange("p n (jb w u) -> p (n jb) u w", w=BLOCK_P, u=2),
         )
-        hs_f32 = keep.tile([P, B_TILES, max(SCALAR_GROUPS) * I_PER_PASS], F32)
-        nc.vector.tensor_copy(out=hs_f32[:], in_=hs_sb[:, :, FIRST_SCALAR_GROUP * I_PER_PASS :])
+        hs_f32 = keep.tile([P, B_TILES, SCALAR_GROUPS * I_PER_PASS], F32)
+        nc.vector.tensor_copy(out=hs_f32[:], in_=hs_sb[:, :, VECTOR_GROUPS * I_PER_PASS :])
 
         def multiply_unit(half, ig, t):
             n = half * TILES_PER_HALF + t
             by_batch = units.tile([P, 2 * J_BLOCKS, I_PER_PASS, 2 * BLOCK_P], BF16)
             for s in range(I_PER_PASS):
-                column = (ig - FIRST_SCALAR_GROUP) * I_PER_PASS + s
+                column = (ig - VECTOR_GROUPS) * I_PER_PASS + s
                 nc.scalar.activation(
                     out=by_batch[:, :, s, :],
                     in_=ht_sorted[:, n],
@@ -200,17 +226,22 @@ def tile_deepandwide_kernel(
 
         out_sb = keep.tile([P, B_TILES, 2 * WIDTH], F32)
         out_rows = out.rearrange("(c n) f -> c n f", n=B_TILES)
-        hsT = keep.tile([P, B_TILES, P], BF16)
         htT = keep.tile([P, B_TILES, P], BF16)
         wlT = keep.tile([P, 2, WIDTH], BF16)
         bias_wide = keep.tile([P, WIDTH], F32)
 
+        def make_bias_wide():
+            bank = psum_work.tile([P, WIDTH], F32, tag="work")
+            nc.tensor.matmul(
+                bank[:], lhsT=ones[:], rhs=bias_rows[:, WIDTH : 2 * WIDTH], start=True, stop=True
+            )
+            nc.scalar.copy(out=bias_wide[:], in_=bank[:])
+
         def prepare_deep_path():
-            for rows, turned in ((hs_sb, hsT), (ht_sb, htT)):
-                bank = psum_work.tile([P, B_TILES, P], BF16, tag="work")
-                for n in range(B_TILES):
-                    nc.tensor.transpose(bank[:, n, :], rows[:, n, :], ident_bf16[:])
-                nc.scalar.copy(out=turned[:], in_=bank[:])
+            bank = psum_work.tile([P, B_TILES, P], BF16, tag="work")
+            for n in range(B_TILES):
+                nc.tensor.transpose(bank[:, n, :], ht_sb[:, n, :], ident_bf16[:])
+            nc.scalar.copy(out=htT[:], in_=bank[:])
             bank = psum_work.tile([P, 2, WIDTH], BF16, tag="work")
             for kh in range(2):
                 for t in range(2):
@@ -218,11 +249,6 @@ def tile_deepandwide_kernel(
                         bank[:, kh, t * P : (t + 1) * P], wl_sb[:, t, kh * P : (kh + 1) * P], ident_bf16[:]
                     )
             nc.scalar.copy(out=wlT[:], in_=bank[:])
-            bank = psum_work.tile([P, WIDTH], F32, tag="work")
-            nc.tensor.matmul(
-                bank[:], lhsT=ones[:], rhs=bias_rows[:, WIDTH : 2 * WIDTH], start=True, stop=True
-            )
-            nc.scalar.copy(out=bias_wide[:], in_=bank[:])
 
         def deep_path(pair):
             bank = psum_work.tile([P, 2, WIDTH], F32, tag="work")
@@ -277,8 +303,8 @@ def tile_deepandwide_kernel(
 
         def contract_step(product, half, ig, jb):
             v_words, v_scales = quantise(product)
-            first_pass = ig == 0 and jb == 0
-            last_pass = ig == I_GROUPS - SCALAR_GROUPS[half] - 1 and jb == J_BLOCKS - 1
+            first_pass = jb == 0 and ig == 0
+            last_pass = jb == J_BLOCKS - 1 and ig == VECTOR_GROUPS - 1
             for t in range(TILES_PER_HALF):
                 if first_pass:
                     acc[(half, t)] = psum_acc.tile([P, WIDTH], F32, name="acc%d" % t)
@@ -296,38 +322,29 @@ def tile_deepandwide_kernel(
                         out=out_rows[:, n, WIDTH : 2 * WIDTH], in_=out_sb[:, n, WIDTH : 2 * WIDTH]
                     )
 
-        later = [lambda jb=jb: make_ht_rows(jb, 1, nc.scalar.copy) for jb in range(J_BLOCKS)]
-        later.append(prepare_deep_path)
+        later = [make_bias_wide, prepare_deep_path]
         later.extend([lambda pair=pair: deep_path(pair) for pair in range(B_TILES // 2)])
-        pieces_done = 0
+        assert len(later) < HALVES * J_BLOCKS
 
         waiting_step = None
-        waiting_unit = None
-        for half in range(HALVES):
-            vector_groups = I_GROUPS - SCALAR_GROUPS[half]
-            for ig in range(vector_groups):
-                for jb in range(J_BLOCKS):
-                    step = ig * J_BLOCKS + jb
-                    if jb == 0:
-                        if ig + 1 < vector_groups:
-                            make_hs_rows(ig + 1, half, nc.scalar.copy)
-                        elif half + 1 < HALVES:
-                            make_hs_rows(0, half + 1, nc.scalar.copy)
-                    started_unit = None
-                    if step % STEPS_PER_UNIT[half] == 0:
-                        group, t = divmod(step // STEPS_PER_UNIT[half], TILES_PER_HALF)
-                        unit_ig = vector_groups + group
-                        started_unit = (multiply_unit(half, unit_ig, t), half, unit_ig, t)
-                    if jb % 2 == 1 and pieces_done < len(later):
-                        later[pieces_done]()
-                        pieces_done += 1
-                    product = multiply_step(half, ig, jb)
-                    if started_unit is not None:
-                        if waiting_unit is not None:
-                            contract_unit(*waiting_unit)
-                        waiting_unit = started_unit
-                    if waiting_step is not None:
-                        contract_step(*waiting_step)
-                    waiting_step = (product, half, ig, jb)
-        contract_unit(*waiting_unit)
+        waiting_units = []
+        for step in range(STEPS):
+            half, jb, ig = place_of(step)
+            build_ahead(step)
+            if step % STEPS_PER_UNIT == 0:
+                scalar_group, t = divmod((step % STEPS_PER_HALF) // STEPS_PER_UNIT, TILES_PER_HALF)
+                unit_ig = VECTOR_GROUPS + scalar_group
+                waiting_units.append((multiply_unit(half, unit_ig, t), half, unit_ig, t))
+            piece = half * J_BLOCKS + jb - 1
+            if ig == VECTOR_GROUPS // 2 and 0 <= piece < len(later):
+                later[piece]()
+            product = multiply_step(half, ig, jb)
+            while len(waiting_units) > UNIT_LAG or waiting_units[0][1] < half:
+                contract_unit(*waiting_units[0])
+                waiting_units = waiting_units[1:]
+            if waiting_step is not None:
+                contract_step(*waiting_step)
+            waiting_step = (product, half, ig, jb)
+        for unit in waiting_units:
+            contract_unit(*unit)
         contract_step(*waiting_step)

@@ -19,29 +19,45 @@ BLOCK_P = 8
 I_PER_PASS = P // BLOCK_P
 I_GROUPS = FEATURES // I_PER_PASS
 J_BLOCKS = FEATURES // (BLOCK_P * PACK)
+PASSES = I_GROUPS * J_BLOCKS
 B_TILES = BATCH // P
 HALVES = 2
-TILES_PER_HALF = B_TILES // HALVES
-HALF_B = TILES_PER_HALF * P
+TILES = B_TILES // HALVES
+HALF_B = TILES * P
 
-SCALAR_GROUPS = 2
-VECTOR_GROUPS = I_GROUPS - SCALAR_GROUPS
-STEPS_PER_UNIT = VECTOR_GROUPS * J_BLOCKS // (SCALAR_GROUPS * TILES_PER_HALF)
-assert STEPS_PER_UNIT * SCALAR_GROUPS * TILES_PER_HALF == VECTOR_GROUPS * J_BLOCKS
-STEPS_PER_HALF = J_BLOCKS * VECTOR_GROUPS
-STEPS = HALVES * STEPS_PER_HALF
-HT_AHEAD = VECTOR_GROUPS
-HST_AHEAD = VECTOR_GROUPS + 2
-HS_AHEAD = 2
-UNIT_LAG = 2
+SHARED_GROUP = 5
+SHARED_TILES = 2
+VECTOR_GROUPS = SHARED_GROUP + 1
+SCALAR_GROUPS = I_GROUPS - SHARED_GROUP
+
+HALF_STEPS = VECTOR_GROUPS * J_BLOCKS
+STEPS = HALVES * HALF_STEPS
+HALF_UNITS = SHARED_TILES + (SCALAR_GROUPS - 1) * TILES
+UNITS = HALVES * HALF_UNITS
+SLOT_STEPS = (15, 7)
 
 FLOPS = 2 * BATCH * FEATURES * FEATURES * WIDTH + 2 * BATCH * 2 * FEATURES * WIDTH
 
 
 def place_of(step):
-    half, rest = divmod(step, STEPS_PER_HALF)
-    jb, ig = divmod(rest, VECTOR_GROUPS)
-    return half, jb, ig
+    half, rest = divmod(step, HALF_STEPS)
+    pair, rest = divmod(rest, 2 * J_BLOCKS)
+    jb, member = divmod(rest, 2)
+    return half, 2 * pair + member, jb
+
+
+def unit_of(unit):
+    half, rest = divmod(unit, HALF_UNITS)
+    group, t = divmod(rest + TILES - SHARED_TILES, TILES)
+    return half, SHARED_GROUP + group, t - (TILES - SHARED_TILES if group == 0 else 0)
+
+
+def first_tile(ig):
+    return SHARED_TILES if ig == SHARED_GROUP else 0
+
+
+def slot_of(unit):
+    return unit * SLOT_STEPS[0] // SLOT_STEPS[1]
 
 
 def tile_deepandwide_kernel(
@@ -51,10 +67,11 @@ def tile_deepandwide_kernel(
     with ExitStack() as ctx:
         keep = ctx.enter_context(tc.tile_pool(name="keep", bufs=1))
         spread = ctx.enter_context(tc.tile_pool(name="spread", bufs=2))
-        units = ctx.enter_context(tc.tile_pool(name="units", bufs=UNIT_LAG + 1))
-        stream = ctx.enter_context(tc.tile_pool(name="stream", bufs=6))
+        units = ctx.enter_context(tc.tile_pool(name="units", bufs=3))
+        stream = ctx.enter_context(tc.tile_pool(name="stream", bufs=8))
         psum_acc = ctx.enter_context(tc.psum_pool(name="psum_acc", bufs=1))
-        psum_work = ctx.enter_context(tc.psum_pool(name="psum_work", bufs=4))
+        psum_hs = ctx.enter_context(tc.psum_pool(name="psum_hs", bufs=2))
+        psum_work = ctx.enter_context(tc.psum_pool(name="psum_work", bufs=2))
 
         ident_bf16 = keep.tile([P, P], BF16)
         make_identity(nc, ident_bf16[:])
@@ -63,10 +80,25 @@ def tile_deepandwide_kernel(
         ones = keep.tile([P, P], BF16)
         nc.gpsimd.memset(ones[:], 1.0)
 
+        ctx.enter_context(
+            tc.manual_schedule(
+                engines={
+                    mybir.EngineType.DVE,
+                    mybir.EngineType.Activation,
+                    mybir.EngineType.Pool,
+                    mybir.EngineType.SP,
+                }
+            )
+        )
+
         hs_sb = keep.tile([P, B_TILES, FEATURES], BF16)
-        nc.sync.dma_start(out=hs_sb[:], in_=hspatial.rearrange("(c n) i -> c n i", n=B_TILES))
         ht_sb = keep.tile([P, B_TILES, FEATURES], BF16)
-        nc.sync.dma_start(out=ht_sb[:], in_=htext.rearrange("(c n) j -> c n j", n=B_TILES))
+        hs_dram = hspatial.rearrange("(c n) i -> c n i", n=B_TILES)
+        ht_dram = htext.rearrange("(c n) j -> c n j", n=B_TILES)
+        for half in range(HALVES):
+            tiles = slice(half * TILES, (half + 1) * TILES)
+            nc.sync.dma_start(out=ht_sb[:, tiles], in_=ht_dram[:, tiles])
+            nc.sync.dma_start(out=hs_sb[:, tiles], in_=hs_dram[:, tiles])
 
         w_scales = keep.tile([P, I_GROUPS, J_BLOCKS, WIDTH], U8, align_bytes=64)
         nc.vector.memset(w_scales[:].rearrange("p a b n -> p (a b n)").bitcast(I32), 0)
@@ -88,66 +120,79 @@ def tile_deepandwide_kernel(
             .rearrange("(ig s jb w) x -> ig jb s w x", ig=I_GROUPS, s=I_PER_PASS, jb=J_BLOCKS, w=BLOCK_P)
         )
         load_order = []
-        for jb in range(J_BLOCKS):
-            load_order.extend([(ig, jb) for ig in range(VECTOR_GROUPS)])
-            if jb < SCALAR_GROUPS:
-                load_order.extend([(VECTOR_GROUPS + jb, other) for other in range(J_BLOCKS)])
-        for ig, jb in load_order:
-            nc.sync.dma_start(out=w_words[:, ig, jb, :].bitcast(I32), in_=word_rows[ig, jb])
+        for step in range(HALF_STEPS):
+            load_order.append(place_of(step)[1:])
+            for unit in range(HALF_UNITS):
+                if slot_of(unit + 2) == step:
+                    load_order.extend([(unit_of(unit)[1], jb) for jb in range(J_BLOCKS)])
+
+        def load_words(count):
+            done = 0
+            while done < count and load_order:
+                ig, jb = load_order[0]
+                load_order.remove((ig, jb))
+                if (ig, jb) not in loaded:
+                    nc.sync.dma_start(out=w_words[:, ig, jb, :].bitcast(I32), in_=word_rows[ig, jb])
+                    loaded[(ig, jb)] = True
+                    done += 1
+
+        loaded = {}
 
         wl_sb = keep.tile([P, 2, 2 * FEATURES], BF16)
-        nc.sync.dma_start(out=wl_sb[:], in_=W_L.rearrange("(t o) k -> o t k", t=2))
         bias_rows = keep.tile([P, 2 * WIDTH], BF16)
         nc.vector.memset(bias_rows[:].bitcast(I32), 0)
-        nc.sync.dma_start(out=bias_rows[0:1, 0:WIDTH], in_=b_L.unsqueeze(0))
-        nc.sync.dma_start(out=bias_rows[0:1, WIDTH : 2 * WIDTH], in_=b_L2.unsqueeze(0))
 
-        hs_rows = keep.tile([P, VECTOR_GROUPS, HALVES, HALF_B * 2], BF16)
-        ht_rows = keep.tile([P, J_BLOCKS, HALVES, HALF_B * PACK], BF16)
-
-
-        hsT = keep.tile([P, B_TILES, P], BF16)
-
-        def make_hsT(half):
-            tiles = slice(half * TILES_PER_HALF, (half + 1) * TILES_PER_HALF)
-            bank = psum_work.tile([P, TILES_PER_HALF, P], BF16, tag="work")
-            for t in range(TILES_PER_HALF):
-                nc.tensor.transpose(bank[:, t, :], hs_sb[:, half * TILES_PER_HALF + t, :], ident_bf16[:])
-            nc.scalar.copy(out=hsT[:, tiles], in_=bank[:])
+        def load_small():
+            nc.sync.dma_start(out=wl_sb[:], in_=W_L.rearrange("(t o) k -> o t k", t=2))
+            nc.sync.dma_start(out=bias_rows[0:1, 0:WIDTH], in_=b_L.unsqueeze(0))
+            nc.sync.dma_start(out=bias_rows[0:1, WIDTH : 2 * WIDTH], in_=b_L2.unsqueeze(0))
 
         choose = keep.tile([P, FEATURES, BLOCK_P], BF16)
         nc.vector.tensor_copy(
             out=choose[:], in_=ident_bf16[:].unsqueeze(2).to_broadcast([P, FEATURES, BLOCK_P])
         )
 
-        def make_hs_rows(ig, half, copy):
-            bank = psum_work.tile([P, 2, 2, P, 2], BF16, tag="work")
-            for k in range(2):
-                first = half * TILES_PER_HALF + 2 * k
-                nc.tensor.matmul(
-                    bank[:, k],
-                    lhsT=choose[:, ig * I_PER_PASS : (ig + 1) * I_PER_PASS, :].rearrange("p s w -> p (s w)"),
-                    rhs=hsT[:, first : first + 2, :].unsqueeze(3).to_broadcast([P, 2, P, 2]),
-                    start=True,
-                    stop=True,
-                )
-            copy(out=hs_rows[:, ig, half, :], in_=bank[:].rearrange("p k n c e -> p (k n c e)"))
+        hsT = keep.tile([P, B_TILES, P], BF16)
 
+        def make_hsT(half):
+            tiles = slice(half * TILES, (half + 1) * TILES)
+            bank = psum_work.tile([P, TILES, P], BF16, tag="work")
+            for t in range(TILES):
+                nc.tensor.transpose(bank[:, t, :], hs_sb[:, half * TILES + t, :], ident_bf16[:])
+            nc.scalar.copy(out=hsT[:, tiles], in_=bank[:])
+
+        def make_hs_bank(ig, half):
+            hs_bank = psum_hs.tile([P, 2, 2, P, 2], BF16)
+            with tc.high_priority():
+                for k in range(first_tile(ig) // 2, 2):
+                    first = half * TILES + 2 * k
+                    nc.tensor.matmul(
+                        hs_bank[:, k],
+                        lhsT=choose[:, ig * I_PER_PASS : (ig + 1) * I_PER_PASS, :].rearrange("p s w -> p (s w)"),
+                        rhs=hsT[:, first : first + 2, :].unsqueeze(3).to_broadcast([P, 2, P, 2]),
+                        start=True,
+                        stop=True,
+                    )
+            return hs_bank
+
+        ht_rows = keep.tile([P, J_BLOCKS, HALVES, HALF_B * PACK], BF16)
         ht_words = ht_sb[:].bitcast(F32)
 
-        def make_ht_rows(jb, half, copy):
-            tiles = slice(half * TILES_PER_HALF, (half + 1) * TILES_PER_HALF)
-            ht_wide = spread.tile([P, 2, TILES_PER_HALF, I_PER_PASS, BLOCK_P], F32)
+        def widen_ht(jb, half, copy):
+            ht_wide = spread.tile([P, 2, TILES, I_PER_PASS, BLOCK_P], F32)
             for u in range(2):
                 words = slice(2 * BLOCK_P * jb + u, 2 * BLOCK_P * (jb + 1), 2)
                 copy(
                     out=ht_wide[:, u],
-                    in_=ht_words[:, tiles, words]
+                    in_=ht_words[:, half * TILES : (half + 1) * TILES, words]
                     .unsqueeze(2)
-                    .to_broadcast([P, TILES_PER_HALF, I_PER_PASS, BLOCK_P]),
+                    .to_broadcast([P, TILES, I_PER_PASS, BLOCK_P]),
                 )
-            for pair in range(TILES_PER_HALF // 2):
-                bank = psum_work.tile([P, 2, 2, P], F32, tag="work")
+            return ht_wide
+
+        def make_ht_rows(jb, half, ht_wide, copies):
+            for pair in range(TILES // 2):
+                bank = psum_acc.tile([P, 2, 2, P], F32, name="acc%d" % pair)
                 for n in range(2):
                     for u in range(2):
                         nc.tensor.transpose(
@@ -156,55 +201,71 @@ def tile_deepandwide_kernel(
                             ident_f32[:],
                         )
                 columns = slice(pair * 2 * P * PACK, (pair + 1) * 2 * P * PACK)
-                copy(
+                copies[pair](
                     out=ht_rows[:, jb, half, columns]
                     .bitcast(F32)
                     .rearrange("p (n c u) -> p n c u", n=2, u=2),
                     in_=bank[:].rearrange("p n u c -> p n c u"),
                 )
 
-        def build_ahead(step):
-            first_use = step + HS_AHEAD
-            if 0 <= first_use < STEPS:
-                half, jb, ig = place_of(first_use)
-                if jb == 0:
-                    make_hs_rows(ig, half, nc.vector.tensor_copy if first_use == 0 else nc.scalar.copy)
-            first_use = step + HT_AHEAD
-            if 0 <= first_use < STEPS:
-                half, jb, ig = place_of(first_use)
-                if ig == 0:
-                    make_ht_rows(jb, half, nc.vector.tensor_copy if first_use == 0 else nc.scalar.copy)
-            first_use = step + HST_AHEAD
-            if 0 <= first_use < STEPS:
-                half, jb, ig = place_of(first_use)
-                if jb == 0 and ig == 0:
-                    make_hsT(half)
+        parked = [
+            out.rearrange("(x r) f -> x r f", r=B_TILES)[: J_BLOCKS * BLOCK_P, 6 - 2 * half : 8 - 2 * half, :]
+            .rearrange("x r f -> x (r f)")
+            for half in range(HALVES)
+        ]
 
-        for step in range(-HST_AHEAD, 0):
-            build_ahead(step)
+        def park_ht(half):
+            bank = psum_work.tile([P, 2, P], F32, tag="work")
+            words = ht_words[:, half * TILES : (half + 1) * TILES, :].rearrange("p n x -> p (n x)")
+            for u in range(2):
+                nc.tensor.transpose(bank[:, u, :], words[:, u::2], ident_f32[:])
+            turned_ht = spread.tile([P, P, 2], F32)
+            nc.scalar.copy(out=turned_ht[:], in_=bank[:].rearrange("p u c -> p c u"))
+            rows = J_BLOCKS * BLOCK_P
+            for n in range(TILES):
+                nc.sync.dma_start(
+                    out=parked[half][:, n * 2 * P : (n + 1) * 2 * P],
+                    in_=turned_ht[n * rows : (n + 1) * rows].rearrange("p c u -> p (c u)"),
+                )
+
+        def fetch_ht(jb, half):
+            rows = parked[half][jb * BLOCK_P : (jb + 1) * BLOCK_P, :]
+            nc.sync.dma_start(
+                out=ht_rows[:, jb, half, :].bitcast(F32),
+                in_=rows.unsqueeze(0).to_broadcast([I_PER_PASS, BLOCK_P, HALF_B * 2]),
+            )
 
         ht_sorted = keep.tile([P, B_TILES, 2 * J_BLOCKS, 2 * BLOCK_P], BF16)
-        nc.vector.tensor_copy(
-            out=ht_sorted[:]
-            .rearrange("p n a x -> p (n a x)")
-            .bitcast(F32)
-            .rearrange("p (m u w) -> p m u w", u=2, w=BLOCK_P),
-            in_=ht_words.rearrange("p n (jb w u) -> p (n jb) u w", w=BLOCK_P, u=2),
-        )
         hs_f32 = keep.tile([P, B_TILES, SCALAR_GROUPS * I_PER_PASS], F32)
-        nc.vector.tensor_copy(out=hs_f32[:], in_=hs_sb[:, :, VECTOR_GROUPS * I_PER_PASS :])
 
-        def multiply_unit(half, ig, t):
-            n = half * TILES_PER_HALF + t
+        def prepare_units(half):
+            tiles = slice(half * TILES, (half + 1) * TILES)
+            nc.vector.tensor_copy(
+                out=ht_sorted[:, tiles]
+                .rearrange("p n a x -> p (n a x)")
+                .bitcast(F32)
+                .rearrange("p (m u w) -> p m u w", u=2, w=BLOCK_P),
+                in_=ht_words[:, tiles].rearrange("p n (jb w u) -> p (n jb) u w", w=BLOCK_P, u=2),
+            )
+            nc.vector.tensor_copy(
+                out=hs_f32[:, tiles], in_=hs_sb[:, tiles, SHARED_GROUP * I_PER_PASS :]
+            )
+
+        def multiply_unit(unit):
+            half, ig, t = unit_of(unit)
+            n = half * TILES + t
             by_batch = units.tile([P, 2 * J_BLOCKS, I_PER_PASS, 2 * BLOCK_P], BF16)
             for s in range(I_PER_PASS):
-                column = (ig - VECTOR_GROUPS) * I_PER_PASS + s
+                column = (ig - SHARED_GROUP) * I_PER_PASS + s
                 nc.scalar.activation(
                     out=by_batch[:, :, s, :],
                     in_=ht_sorted[:, n],
                     func=mybir.ActivationFunctionType.Copy,
                     scale=hs_f32[:, n, column : column + 1],
                 )
+            return by_batch
+
+        def turn_unit(by_batch):
             unit_product = units.tile([P, J_BLOCKS * P * PACK], BF16, align_bytes=64)
             for pair in range(J_BLOCKS // 2):
                 bank = psum_work.tile([P, 2, 2, P], F32, tag="work")
@@ -237,11 +298,13 @@ def tile_deepandwide_kernel(
             )
             nc.scalar.copy(out=bias_wide[:], in_=bank[:])
 
-        def prepare_deep_path():
+        def make_htT():
             bank = psum_work.tile([P, B_TILES, P], BF16, tag="work")
             for n in range(B_TILES):
                 nc.tensor.transpose(bank[:, n, :], ht_sb[:, n, :], ident_bf16[:])
             nc.scalar.copy(out=htT[:], in_=bank[:])
+
+        def make_wlT():
             bank = psum_work.tile([P, 2, WIDTH], BF16, tag="work")
             for kh in range(2):
                 for t in range(2):
@@ -264,87 +327,133 @@ def tile_deepandwide_kernel(
             )
 
         def quantise(operand):
-            v_words = stream.tile([P, HALF_B], U32, align_bytes=64)
-            v_scales = stream.tile([P, HALF_B], U8, align_bytes=64)
+            v_words = stream.tile([P, operand.shape[1] // PACK], U32, align_bytes=64)
+            v_scales = stream.tile([P, operand.shape[1] // PACK], U8, align_bytes=64)
             nc.vector.quantize_mx(out=v_words[:].bitcast(FP8X4), scales=v_scales[:], in_=operand[:])
             return v_words, v_scales
 
-        def contract(total, v_words, v_scales, piece, ig, jb, start, stop):
-            columns = slice(piece * P, (piece + 1) * P)
-            nc.tensor.matmul_mx(
-                out=total[:],
-                lhsT=v_words[:, columns].bitcast(FP8X4),
-                lhsT_scale=v_scales[:, columns],
-                rhs=w_words[:, ig, jb, :].bitcast(FP8X4),
-                rhs_scale=w_scales[:, ig, jb, :],
-                start=start,
-                stop=stop,
-            )
-
-        def multiply_step(half, ig, jb):
-            product = stream.tile([P, HALF_B * PACK], BF16, align_bytes=64)
+        def multiply_step(half, ig, jb, hs_bank):
+            first = first_tile(ig) * P
+            rows = HALF_B - first
+            product = stream.tile([P, rows * PACK], BF16, align_bytes=64)
             nc.vector.tensor_tensor(
                 out=product[:].rearrange("p (b u e) -> p b u e", u=2, e=2),
-                in0=ht_rows[:, jb, half, :].rearrange("p (b u e) -> p b u e", u=2, e=2),
-                in1=hs_rows[:, ig, half, :]
-                .rearrange("p (b e) -> p b e", e=2)
+                in0=ht_rows[:, jb, half, first * PACK :].rearrange("p (b u e) -> p b u e", u=2, e=2),
+                in1=hs_bank[:]
+                .rearrange("p k n c e -> p (k n c) e")[:, first:, :]
                 .unsqueeze(2)
-                .to_broadcast([P, HALF_B, 2, 2]),
+                .to_broadcast([P, rows, 2, 2]),
                 op=mybir.AluOpType.mult,
             )
             return product
 
         acc = {}
+        added = {}
 
-        def contract_unit(unit_product, half, ig, t):
-            v_words, v_scales = quantise(unit_product)
-            for jb in range(J_BLOCKS):
-                contract(acc[(half, t)], v_words, v_scales, jb, ig, jb, False, False)
+        def contract(quantised, piece, half, t, ig, jb):
+            v_words, v_scales = quantised
+            count = added.get((half, t), 0)
+            if count == 0:
+                acc[(half, t)] = psum_acc.tile([P, WIDTH], F32, name="acc%d" % t)
+            columns = slice(piece * P, (piece + 1) * P)
+            nc.tensor.matmul_mx(
+                out=acc[(half, t)][:],
+                lhsT=v_words[:, columns].bitcast(FP8X4),
+                lhsT_scale=v_scales[:, columns],
+                rhs=w_words[:, ig, jb, :].bitcast(FP8X4),
+                rhs_scale=w_scales[:, ig, jb, :],
+                start=count == 0,
+                stop=count == PASSES - 1,
+            )
+            added[(half, t)] = count + 1
 
-        def contract_step(product, half, ig, jb):
-            v_words, v_scales = quantise(product)
-            first_pass = jb == 0 and ig == 0
-            last_pass = jb == J_BLOCKS - 1 and ig == VECTOR_GROUPS - 1
-            for t in range(TILES_PER_HALF):
-                if first_pass:
-                    acc[(half, t)] = psum_acc.tile([P, WIDTH], F32, name="acc%d" % t)
-                contract(acc[(half, t)], v_words, v_scales, t, ig, jb, first_pass, last_pass)
-            if last_pass:
-                for t in range(TILES_PER_HALF):
-                    n = half * TILES_PER_HALF + t
-                    nc.vector.tensor_tensor(
-                        out=out_sb[:, n, WIDTH : 2 * WIDTH],
-                        in0=acc[(half, t)][:],
-                        in1=bias_wide[:],
-                        op=mybir.AluOpType.add,
-                    )
-                    nc.sync.dma_start(
-                        out=out_rows[:, n, WIDTH : 2 * WIDTH], in_=out_sb[:, n, WIDTH : 2 * WIDTH]
-                    )
+        def store_half(half):
+            for t in range(TILES):
+                n = half * TILES + t
+                nc.vector.tensor_tensor(
+                    out=out_sb[:, n, WIDTH : 2 * WIDTH],
+                    in0=acc[(half, t)][:],
+                    in1=bias_wide[:],
+                    op=mybir.AluOpType.add,
+                )
+                nc.sync.dma_start(
+                    out=out_rows[:, n, WIDTH : 2 * WIDTH], in_=out_sb[:, n, WIDTH : 2 * WIDTH]
+                )
 
-        later = [make_bias_wide, prepare_deep_path]
-        later.extend([lambda pair=pair: deep_path(pair) for pair in range(B_TILES // 2)])
-        assert len(later) < HALVES * J_BLOCKS
+        make_hsT(0)
+        wide = widen_ht(0, 0, nc.vector.tensor_copy)
+        park_ht(0)
+        load_words(4)
+        hs_banks = {(0, 0): make_hs_bank(0, 0)}
+        make_ht_rows(0, 0, wide, (nc.vector.tensor_copy, nc.scalar.copy))
+        for jb in range(1, J_BLOCKS):
+            fetch_ht(jb, 0)
+            load_words(4)
+        prepare_units(0)
+        hs_banks[(1, 0)] = make_hs_bank(1, 0)
+        load_words(PASSES)
+        load_small()
 
-        waiting_step = None
-        waiting_units = []
-        for step in range(STEPS):
-            half, jb, ig = place_of(step)
-            build_ahead(step)
-            if step % STEPS_PER_UNIT == 0:
-                scalar_group, t = divmod((step % STEPS_PER_HALF) // STEPS_PER_UNIT, TILES_PER_HALF)
-                unit_ig = VECTOR_GROUPS + scalar_group
-                waiting_units.append((multiply_unit(half, unit_ig, t), half, unit_ig, t))
-            piece = half * J_BLOCKS + jb - 1
-            if ig == VECTOR_GROUPS // 2 and 0 <= piece < len(later):
-                later[piece]()
-            product = multiply_step(half, ig, jb)
-            while len(waiting_units) > UNIT_LAG or waiting_units[0][1] < half:
-                contract_unit(*waiting_units[0])
-                waiting_units = waiting_units[1:]
-            if waiting_step is not None:
-                contract_step(*waiting_step)
-            waiting_step = (product, half, ig, jb)
-        for unit in waiting_units:
-            contract_unit(*unit)
-        contract_step(*waiting_step)
+        todo = {}
+
+        def at(step, work):
+            todo.setdefault(step, []).append(work)
+
+        at(6, lambda: prepare_units(1))
+        at(7, lambda: make_hsT(1))
+        at(8, lambda: park_ht(1))
+        for jb in range(J_BLOCKS):
+            at(9, lambda jb=jb: fetch_ht(jb, 1))
+        at(HALF_STEPS - 5, make_bias_wide)
+        at(HALF_STEPS + 7, make_htT)
+        at(HALF_STEPS + 8, make_wlT)
+        for pair in range(B_TILES // 2):
+            at(HALF_STEPS + 10 + 2 * pair, lambda pair=pair: deep_path(pair))
+
+        products = {}
+        by_batch = {}
+        turned = {}
+        ready = []
+        open_half = 0
+
+        for step in range(STEPS + 1):
+            for work in todo.get(step, []):
+                work()
+            quantise_units = []
+            for unit in range(UNITS + 2):
+                if slot_of(unit) != step:
+                    continue
+                if unit < UNITS:
+                    by_batch[unit] = multiply_unit(unit)
+                if 0 <= unit - 1 < UNITS:
+                    turned[unit - 1] = turn_unit(by_batch[unit - 1])
+                if unit - 2 >= 0:
+                    quantise_units.append(unit - 2)
+            if step < STEPS:
+                half, ig, jb = place_of(step)
+                products[step] = multiply_step(half, ig, jb, hs_banks[(ig, half)])
+            for unit in quantise_units:
+                half, ig, t = unit_of(unit)
+                quantised = quantise(turned[unit])
+                ready.append((half, [(quantised, jb, half, t, ig, jb) for jb in range(J_BLOCKS)]))
+            if step - 1 in products:
+                half, ig, jb = place_of(step - 1)
+                quantised = quantise(products[step - 1])
+                first = first_tile(ig)
+                ready.append((half, [(quantised, t - first, half, t, ig, jb) for t in range(first, TILES)]))
+            held = []
+            for half, passes in ready:
+                if half != open_half:
+                    held.append((half, passes))
+                    continue
+                for one in passes:
+                    contract(*one)
+            ready = held
+            if all([added.get((open_half, t), 0) == PASSES for t in range(TILES)]):
+                store_half(open_half)
+                open_half += 1
+            ahead = step + 2
+            if 2 <= ahead < STEPS:
+                half, ig, jb = place_of(ahead)
+                if (ig, half) not in hs_banks:
+                    hs_banks[(ig, half)] = make_hs_bank(ig, half)

@@ -95,10 +95,13 @@ def tile_deepandwide_kernel(
         ht_sb = keep.tile([P, B_TILES, FEATURES], BF16)
         hs_dram = hspatial.rearrange("(c n) i -> c n i", n=B_TILES)
         ht_dram = htext.rearrange("(c n) j -> c n j", n=B_TILES)
-        for half in range(HALVES):
+
+        def load_half(half):
             tiles = slice(half * TILES, (half + 1) * TILES)
             nc.sync.dma_start(out=ht_sb[:, tiles], in_=ht_dram[:, tiles])
             nc.sync.dma_start(out=hs_sb[:, tiles], in_=hs_dram[:, tiles])
+
+        load_half(0)
 
         w_scales = keep.tile([P, I_GROUPS, J_BLOCKS, WIDTH], U8, align_bytes=64)
         nc.vector.memset(w_scales[:].rearrange("p a b n -> p (a b n)").bitcast(I32), 0)
@@ -126,26 +129,21 @@ def tile_deepandwide_kernel(
                 if slot_of(unit + 2) == step:
                     load_order.extend([(unit_of(unit)[1], jb) for jb in range(J_BLOCKS)])
 
-        def load_words(count):
-            done = 0
-            while done < count and load_order:
-                ig, jb = load_order[0]
-                load_order.remove((ig, jb))
-                if (ig, jb) not in loaded:
-                    nc.sync.dma_start(out=w_words[:, ig, jb, :].bitcast(I32), in_=word_rows[ig, jb])
-                    loaded[(ig, jb)] = True
-                    done += 1
-
         loaded = {}
+        for ig, jb in load_order:
+            if (ig, jb) in loaded:
+                continue
+            nc.sync.dma_start(out=w_words[:, ig, jb, :].bitcast(I32), in_=word_rows[ig, jb])
+            loaded[(ig, jb)] = True
+            if len(loaded) == PASSES // 2:
+                load_half(1)
 
         wl_sb = keep.tile([P, 2, 2 * FEATURES], BF16)
         bias_rows = keep.tile([P, 2 * WIDTH], BF16)
         nc.vector.memset(bias_rows[:].bitcast(I32), 0)
-
-        def load_small():
-            nc.sync.dma_start(out=wl_sb[:], in_=W_L.rearrange("(t o) k -> o t k", t=2))
-            nc.sync.dma_start(out=bias_rows[0:1, 0:WIDTH], in_=b_L.unsqueeze(0))
-            nc.sync.dma_start(out=bias_rows[0:1, WIDTH : 2 * WIDTH], in_=b_L2.unsqueeze(0))
+        nc.sync.dma_start(out=wl_sb[:], in_=W_L.rearrange("(t o) k -> o t k", t=2))
+        nc.sync.dma_start(out=bias_rows[0:1, 0:WIDTH], in_=b_L.unsqueeze(0))
+        nc.sync.dma_start(out=bias_rows[0:1, WIDTH : 2 * WIDTH], in_=b_L2.unsqueeze(0))
 
         choose = keep.tile([P, FEATURES, BLOCK_P], BF16)
         nc.vector.tensor_copy(
@@ -192,7 +190,10 @@ def tile_deepandwide_kernel(
 
         def make_ht_rows(jb, half, ht_wide, copies):
             for pair in range(TILES // 2):
-                bank = psum_acc.tile([P, 2, 2, P], F32, name="acc%d" % pair)
+                if jb < 2:
+                    bank = psum_acc.tile([P, 2, 2, P], F32, name="acc%d" % (2 * jb + pair))
+                else:
+                    bank = psum_work.tile([P, 2, 2, P], F32, tag="work")
                 for n in range(2):
                     for u in range(2):
                         nc.tensor.transpose(
@@ -208,15 +209,14 @@ def tile_deepandwide_kernel(
                     in_=bank[:].rearrange("p n u c -> p n c u"),
                 )
 
-        parked = [
-            out.rearrange("(x r) f -> x r f", r=B_TILES)[: J_BLOCKS * BLOCK_P, 6 - 2 * half : 8 - 2 * half, :]
+        parked = (
+            out.rearrange("(x r) f -> x r f", r=B_TILES)[: J_BLOCKS * BLOCK_P, 4:6, :]
             .rearrange("x r f -> x (r f)")
-            for half in range(HALVES)
-        ]
+        )
 
-        def park_ht(half):
+        def park_ht():
             bank = psum_work.tile([P, 2, P], F32, tag="work")
-            words = ht_words[:, half * TILES : (half + 1) * TILES, :].rearrange("p n x -> p (n x)")
+            words = ht_words[:, TILES:, :].rearrange("p n x -> p (n x)")
             for u in range(2):
                 nc.tensor.transpose(bank[:, u, :], words[:, u::2], ident_f32[:])
             turned_ht = spread.tile([P, P, 2], F32)
@@ -224,14 +224,14 @@ def tile_deepandwide_kernel(
             rows = J_BLOCKS * BLOCK_P
             for n in range(TILES):
                 nc.sync.dma_start(
-                    out=parked[half][:, n * 2 * P : (n + 1) * 2 * P],
+                    out=parked[:, n * 2 * P : (n + 1) * 2 * P],
                     in_=turned_ht[n * rows : (n + 1) * rows].rearrange("p c u -> p (c u)"),
                 )
 
-        def fetch_ht(jb, half):
-            rows = parked[half][jb * BLOCK_P : (jb + 1) * BLOCK_P, :]
+        def fetch_ht(jb):
+            rows = parked[jb * BLOCK_P : (jb + 1) * BLOCK_P, :]
             nc.sync.dma_start(
-                out=ht_rows[:, jb, half, :].bitcast(F32),
+                out=ht_rows[:, jb, 1, :].bitcast(F32),
                 in_=rows.unsqueeze(0).to_broadcast([I_PER_PASS, BLOCK_P, HALF_B * 2]),
             )
 
@@ -381,18 +381,15 @@ def tile_deepandwide_kernel(
                 )
 
         make_hsT(0)
-        wide = widen_ht(0, 0, nc.vector.tensor_copy)
-        park_ht(0)
-        load_words(4)
+        wide = {0: widen_ht(0, 0, nc.vector.tensor_copy)}
         hs_banks = {(0, 0): make_hs_bank(0, 0)}
-        make_ht_rows(0, 0, wide, (nc.vector.tensor_copy, nc.scalar.copy))
-        for jb in range(1, J_BLOCKS):
-            fetch_ht(jb, 0)
-            load_words(4)
+        wide[1] = widen_ht(1, 0, nc.vector.tensor_copy)
+        make_ht_rows(0, 0, wide[0], (nc.vector.tensor_copy, nc.scalar.copy))
         prepare_units(0)
         hs_banks[(1, 0)] = make_hs_bank(1, 0)
-        load_words(PASSES)
-        load_small()
+        by_scalar = (nc.scalar.copy, nc.scalar.copy)
+        make_ht_rows(1, 0, wide[1], by_scalar)
+        wide[2] = widen_ht(2, 0, nc.scalar.copy)
 
         todo = {}
 
@@ -401,9 +398,16 @@ def tile_deepandwide_kernel(
 
         at(6, lambda: prepare_units(1))
         at(7, lambda: make_hsT(1))
-        at(8, lambda: park_ht(1))
+        def next_ht(jb):
+            make_ht_rows(jb, 0, wide[jb], by_scalar)
+            if jb + 1 < J_BLOCKS:
+                wide[jb + 1] = widen_ht(jb + 1, 0, nc.scalar.copy)
+
+        at(1, lambda: next_ht(2))
+        at(3, lambda: next_ht(3))
+        at(8, park_ht)
         for jb in range(J_BLOCKS):
-            at(9, lambda jb=jb: fetch_ht(jb, 1))
+            at(9, lambda jb=jb: fetch_ht(jb))
         at(HALF_STEPS - 5, make_bias_wide)
         at(HALF_STEPS + 7, make_htT)
         at(HALF_STEPS + 8, make_wlT)

@@ -34,6 +34,7 @@ HALF_STEPS = VECTOR_GROUPS * J_BLOCKS
 STEPS = HALVES * HALF_STEPS
 HALF_UNITS = SHARED_TILES + (SCALAR_GROUPS - 1) * TILES
 UNITS = HALVES * HALF_UNITS
+FIRST_SLOT = 1
 SLOT_STEPS = (15, 7)
 
 FLOPS = 2 * BATCH * FEATURES * FEATURES * WIDTH + 2 * BATCH * 2 * FEATURES * WIDTH
@@ -57,7 +58,7 @@ def first_tile(ig):
 
 
 def slot_of(unit):
-    return unit * SLOT_STEPS[0] // SLOT_STEPS[1]
+    return FIRST_SLOT + unit * SLOT_STEPS[0] // SLOT_STEPS[1]
 
 
 def tile_deepandwide_kernel(
@@ -70,8 +71,7 @@ def tile_deepandwide_kernel(
         units = ctx.enter_context(tc.tile_pool(name="units", bufs=3))
         stream = ctx.enter_context(tc.tile_pool(name="stream", bufs=8))
         psum_acc = ctx.enter_context(tc.psum_pool(name="psum_acc", bufs=1))
-        psum_hs = ctx.enter_context(tc.psum_pool(name="psum_hs", bufs=2))
-        psum_work = ctx.enter_context(tc.psum_pool(name="psum_work", bufs=2))
+        psum_work = ctx.enter_context(tc.psum_pool(name="psum_work", bufs=4))
 
         ident_bf16 = keep.tile([P, P], BF16)
         make_identity(nc, ident_bf16[:])
@@ -79,17 +79,6 @@ def tile_deepandwide_kernel(
         make_identity(nc, ident_f32[:])
         ones = keep.tile([P, P], BF16)
         nc.gpsimd.memset(ones[:], 1.0)
-
-        ctx.enter_context(
-            tc.manual_schedule(
-                engines={
-                    mybir.EngineType.DVE,
-                    mybir.EngineType.Activation,
-                    mybir.EngineType.Pool,
-                    mybir.EngineType.SP,
-                }
-            )
-        )
 
         hs_sb = keep.tile([P, B_TILES, FEATURES], BF16)
         ht_sb = keep.tile([P, B_TILES, FEATURES], BF16)
@@ -101,20 +90,20 @@ def tile_deepandwide_kernel(
             nc.sync.dma_start(out=ht_sb[:, tiles], in_=ht_dram[:, tiles])
             nc.sync.dma_start(out=hs_sb[:, tiles], in_=hs_dram[:, tiles])
 
-        load_half(0)
-
         w_scales = keep.tile([P, I_GROUPS, J_BLOCKS, WIDTH], U8, align_bytes=64)
-        nc.vector.memset(w_scales[:].rearrange("p a b n -> p (a b n)").bitcast(I32), 0)
         scale_rows = (
             W_L2_scales.rearrange("g q n -> (g q) n")
             .rearrange("(ig Q r jb) n -> Q r ig (jb n)", ig=I_GROUPS, Q=4, r=4, jb=J_BLOCKS)
             .bitcast(I32)
         )
-        for Q in range(4):
-            nc.sync.dma_start(
-                out=w_scales[32 * Q : 32 * Q + 4].rearrange("r a b n -> r a (b n)").bitcast(I32),
-                in_=scale_rows[Q],
-            )
+
+        def load_scales():
+            nc.vector.memset(w_scales[:].rearrange("p a b n -> p (a b n)").bitcast(I32), 0)
+            for Q in range(4):
+                nc.sync.dma_start(
+                    out=w_scales[32 * Q : 32 * Q + 4].rearrange("r a b n -> r a (b n)").bitcast(I32),
+                    in_=scale_rows[Q],
+                )
 
         w_words = keep.tile([P, I_GROUPS, J_BLOCKS, WIDTH], U32, align_bytes=64)
         word_rows = (
@@ -130,48 +119,64 @@ def tile_deepandwide_kernel(
                     load_order.extend([(unit_of(unit)[1], jb) for jb in range(J_BLOCKS)])
 
         loaded = {}
-        for ig, jb in load_order:
-            if (ig, jb) in loaded:
-                continue
-            nc.sync.dma_start(out=w_words[:, ig, jb, :].bitcast(I32), in_=word_rows[ig, jb])
-            loaded[(ig, jb)] = True
-            if len(loaded) == PASSES // 2:
-                load_half(1)
+
+        def load_words(count):
+            goal = len(loaded) + count
+            for ig, jb in load_order:
+                if (ig, jb) not in loaded and len(loaded) < goal:
+                    nc.sync.dma_start(out=w_words[:, ig, jb, :].bitcast(I32), in_=word_rows[ig, jb])
+                    loaded[(ig, jb)] = True
 
         wl_sb = keep.tile([P, 2, 2 * FEATURES], BF16)
         bias_rows = keep.tile([P, 2 * WIDTH], BF16)
-        nc.vector.memset(bias_rows[:].bitcast(I32), 0)
-        nc.sync.dma_start(out=wl_sb[:], in_=W_L.rearrange("(t o) k -> o t k", t=2))
-        nc.sync.dma_start(out=bias_rows[0:1, 0:WIDTH], in_=b_L.unsqueeze(0))
-        nc.sync.dma_start(out=bias_rows[0:1, WIDTH : 2 * WIDTH], in_=b_L2.unsqueeze(0))
+
+        def load_small():
+            nc.vector.memset(bias_rows[:].bitcast(I32), 0)
+            nc.sync.dma_start(out=wl_sb[:], in_=W_L.rearrange("(t o) k -> o t k", t=2))
+            nc.sync.dma_start(out=bias_rows[0:1, 0:WIDTH], in_=b_L.unsqueeze(0))
+            nc.sync.dma_start(out=bias_rows[0:1, WIDTH : 2 * WIDTH], in_=b_L2.unsqueeze(0))
 
         choose = keep.tile([P, FEATURES, BLOCK_P], BF16)
-        nc.vector.tensor_copy(
-            out=choose[:], in_=ident_bf16[:].unsqueeze(2).to_broadcast([P, FEATURES, BLOCK_P])
-        )
 
         hsT = keep.tile([P, B_TILES, P], BF16)
+        hs_pairs = keep.tile([P, B_TILES, P, 2], BF16)
+        hs_rows = keep.tile([P, VECTOR_GROUPS, HALVES, HALF_B * 2], BF16)
 
-        def make_hsT(half):
-            tiles = slice(half * TILES, (half + 1) * TILES)
+        def turn_hs(half):
             bank = psum_work.tile([P, TILES, P], BF16, tag="work")
             for t in range(TILES):
                 nc.tensor.transpose(bank[:, t, :], hs_sb[:, half * TILES + t, :], ident_bf16[:])
-            nc.scalar.copy(out=hsT[:, tiles], in_=bank[:])
+            nc.scalar.copy(out=hsT[:, half * TILES : (half + 1) * TILES], in_=bank[:])
+            return bank
 
-        def make_hs_bank(ig, half):
-            hs_bank = psum_hs.tile([P, 2, 2, P, 2], BF16)
-            with tc.high_priority():
-                for k in range(first_tile(ig) // 2, 2):
-                    first = half * TILES + 2 * k
-                    nc.tensor.matmul(
-                        hs_bank[:, k],
-                        lhsT=choose[:, ig * I_PER_PASS : (ig + 1) * I_PER_PASS, :].rearrange("p s w -> p (s w)"),
-                        rhs=hsT[:, first : first + 2, :].unsqueeze(3).to_broadcast([P, 2, P, 2]),
-                        start=True,
-                        stop=True,
-                    )
-            return hs_bank
+        def make_hs_rows(ig, half):
+            bank = psum_work.tile([P, 2, 2, P, 2], BF16, tag="work")
+            for k in range(2):
+                first = half * TILES + 2 * k
+                nc.tensor.matmul(
+                    bank[:, k],
+                    lhsT=choose[:, ig * I_PER_PASS : (ig + 1) * I_PER_PASS, :].rearrange("p s w -> p (s w)"),
+                    rhs=hsT[:, first : first + 2, :].unsqueeze(3).to_broadcast([P, 2, P, 2]),
+                    start=True,
+                    stop=True,
+                )
+            nc.scalar.copy(out=hs_rows[:, ig, half, :], in_=bank[:].rearrange("p k n c e -> p (k n c e)"))
+
+        parked_hs = [out.rearrange("(i r) f -> i r f", r=B_TILES)[:, 6 + half, :] for half in range(HALVES)]
+
+        def park_hs(half, bank):
+            tiles = slice(half * TILES, (half + 1) * TILES)
+            nc.scalar.copy(out=hs_pairs[:, tiles], in_=bank[:].unsqueeze(3).to_broadcast([P, TILES, P, 2]))
+            nc.scalar.dma_start(
+                out=parked_hs[half], in_=hs_pairs[:, tiles].rearrange("p n c e -> p (n c e)").bitcast(F32)
+            )
+
+        def fetch_hs(ig, half):
+            rows = parked_hs[half][ig * I_PER_PASS : (ig + 1) * I_PER_PASS, :]
+            nc.sync.dma_start(
+                out=hs_rows[:, ig, half, :].bitcast(F32),
+                in_=rows.unsqueeze(1).to_broadcast([I_PER_PASS, BLOCK_P, HALF_B]),
+            )
 
         ht_rows = keep.tile([P, J_BLOCKS, HALVES, HALF_B * PACK], BF16)
         ht_words = ht_sb[:].bitcast(F32)
@@ -190,10 +195,7 @@ def tile_deepandwide_kernel(
 
         def make_ht_rows(jb, half, ht_wide, copies):
             for pair in range(TILES // 2):
-                if jb < 2:
-                    bank = psum_acc.tile([P, 2, 2, P], F32, name="acc%d" % (2 * jb + pair))
-                else:
-                    bank = psum_work.tile([P, 2, 2, P], F32, tag="work")
+                bank = psum_acc.tile([P, 2, 2, P], F32, name="acc%d" % (2 * jb + pair))
                 for n in range(2):
                     for u in range(2):
                         nc.tensor.transpose(
@@ -209,29 +211,30 @@ def tile_deepandwide_kernel(
                     in_=bank[:].rearrange("p n u c -> p n c u"),
                 )
 
-        parked = (
-            out.rearrange("(x r) f -> x r f", r=B_TILES)[: J_BLOCKS * BLOCK_P, 4:6, :]
+        parked_ht = [
+            out.rearrange("(x r) f -> x r f", r=B_TILES)[: J_BLOCKS * BLOCK_P, 2 + 2 * half : 4 + 2 * half, :]
             .rearrange("x r f -> x (r f)")
-        )
+            for half in range(HALVES)
+        ]
 
-        def park_ht():
+        def park_ht(half):
             bank = psum_work.tile([P, 2, P], F32, tag="work")
-            words = ht_words[:, TILES:, :].rearrange("p n x -> p (n x)")
+            words = ht_words[:, half * TILES : (half + 1) * TILES, :].rearrange("p n x -> p (n x)")
             for u in range(2):
                 nc.tensor.transpose(bank[:, u, :], words[:, u::2], ident_f32[:])
             turned_ht = spread.tile([P, P, 2], F32)
             nc.scalar.copy(out=turned_ht[:], in_=bank[:].rearrange("p u c -> p c u"))
             rows = J_BLOCKS * BLOCK_P
             for n in range(TILES):
-                nc.sync.dma_start(
-                    out=parked[:, n * 2 * P : (n + 1) * 2 * P],
+                nc.scalar.dma_start(
+                    out=parked_ht[half][:, n * 2 * P : (n + 1) * 2 * P],
                     in_=turned_ht[n * rows : (n + 1) * rows].rearrange("p c u -> p (c u)"),
                 )
 
-        def fetch_ht(jb):
-            rows = parked[jb * BLOCK_P : (jb + 1) * BLOCK_P, :]
+        def fetch_ht(jb, half):
+            rows = parked_ht[half][jb * BLOCK_P : (jb + 1) * BLOCK_P, :]
             nc.sync.dma_start(
-                out=ht_rows[:, jb, 1, :].bitcast(F32),
+                out=ht_rows[:, jb, half, :].bitcast(F32),
                 in_=rows.unsqueeze(0).to_broadcast([I_PER_PASS, BLOCK_P, HALF_B * 2]),
             )
 
@@ -332,15 +335,15 @@ def tile_deepandwide_kernel(
             nc.vector.quantize_mx(out=v_words[:].bitcast(FP8X4), scales=v_scales[:], in_=operand[:])
             return v_words, v_scales
 
-        def multiply_step(half, ig, jb, hs_bank):
+        def multiply_step(half, ig, jb):
             first = first_tile(ig) * P
             rows = HALF_B - first
             product = stream.tile([P, rows * PACK], BF16, align_bytes=64)
             nc.vector.tensor_tensor(
                 out=product[:].rearrange("p (b u e) -> p b u e", u=2, e=2),
                 in0=ht_rows[:, jb, half, first * PACK :].rearrange("p (b u e) -> p b u e", u=2, e=2),
-                in1=hs_bank[:]
-                .rearrange("p k n c e -> p (k n c) e")[:, first:, :]
+                in1=hs_rows[:, ig, half, first * 2 :]
+                .rearrange("p (b e) -> p b e", e=2)
                 .unsqueeze(2)
                 .to_broadcast([P, rows, 2, 2]),
                 op=mybir.AluOpType.mult,
@@ -380,34 +383,60 @@ def tile_deepandwide_kernel(
                     out=out_rows[:, n, WIDTH : 2 * WIDTH], in_=out_sb[:, n, WIDTH : 2 * WIDTH]
                 )
 
-        make_hsT(0)
-        wide = {0: widen_ht(0, 0, nc.vector.tensor_copy)}
-        hs_banks = {(0, 0): make_hs_bank(0, 0)}
-        wide[1] = widen_ht(1, 0, nc.vector.tensor_copy)
-        make_ht_rows(0, 0, wide[0], (nc.vector.tensor_copy, nc.scalar.copy))
-        prepare_units(0)
-        hs_banks[(1, 0)] = make_hs_bank(1, 0)
-        by_scalar = (nc.scalar.copy, nc.scalar.copy)
-        make_ht_rows(1, 0, wide[1], by_scalar)
-        wide[2] = widen_ht(2, 0, nc.scalar.copy)
+        with tc.manual_schedule():
+            load_half(0)
+            load_scales()
+            load_words(4)
+            hs_bank = turn_hs(0)
+            nc.vector.tensor_copy(
+                out=choose[:], in_=ident_bf16[:].unsqueeze(2).to_broadcast([P, FEATURES, BLOCK_P])
+            )
+            ht_wide = widen_ht(0, 0, nc.vector.tensor_copy)
+            make_ht_rows(0, 0, ht_wide, (nc.vector.tensor_copy, nc.vector.tensor_copy))
+            make_hs_rows(0, 0)
+            park_ht(0)
+            ht_wide = widen_ht(1, 0, nc.vector.tensor_copy)
+            make_hs_rows(1, 0)
+            make_ht_rows(1, 0, ht_wide, (nc.scalar.copy, nc.scalar.copy))
+            park_hs(0, hs_bank)
+            prepare_units(0)
+            load_words(2)
+            for jb in range(2, J_BLOCKS):
+                fetch_ht(jb, 0)
+                load_words(2)
+            for ig in range(2, VECTOR_GROUPS):
+                fetch_hs(ig, 0)
+                load_words(4)
+            load_half(1)
+            load_words(PASSES)
+            load_small()
+
+        ctx.enter_context(
+            tc.manual_schedule(
+                engines={
+                    mybir.EngineType.DVE,
+                    mybir.EngineType.Activation,
+                    mybir.EngineType.Pool,
+                    mybir.EngineType.SP,
+                }
+            )
+        )
 
         todo = {}
 
         def at(step, work):
             todo.setdefault(step, []).append(work)
 
-        at(6, lambda: prepare_units(1))
-        at(7, lambda: make_hsT(1))
-        def next_ht(jb):
-            make_ht_rows(jb, 0, wide[jb], by_scalar)
-            if jb + 1 < J_BLOCKS:
-                wide[jb + 1] = widen_ht(jb + 1, 0, nc.scalar.copy)
+        def second_half():
+            prepare_units(1)
+            park_ht(1)
+            park_hs(1, turn_hs(1))
+            for jb in range(J_BLOCKS):
+                fetch_ht(jb, 1)
+            for ig in range(VECTOR_GROUPS):
+                fetch_hs(ig, 1)
 
-        at(1, lambda: next_ht(2))
-        at(3, lambda: next_ht(3))
-        at(8, park_ht)
-        for jb in range(J_BLOCKS):
-            at(9, lambda jb=jb: fetch_ht(jb))
+        at(10, second_half)
         at(HALF_STEPS - 5, make_bias_wide)
         at(HALF_STEPS + 7, make_htT)
         at(HALF_STEPS + 8, make_wlT)
@@ -435,7 +464,7 @@ def tile_deepandwide_kernel(
                     quantise_units.append(unit - 2)
             if step < STEPS:
                 half, ig, jb = place_of(step)
-                products[step] = multiply_step(half, ig, jb, hs_banks[(ig, half)])
+                products[step] = multiply_step(half, ig, jb)
             for unit in quantise_units:
                 half, ig, t = unit_of(unit)
                 quantised = quantise(turned[unit])
@@ -456,8 +485,3 @@ def tile_deepandwide_kernel(
             if all([added.get((open_half, t), 0) == PASSES for t in range(TILES)]):
                 store_half(open_half)
                 open_half += 1
-            ahead = step + 2
-            if 2 <= ahead < STEPS:
-                half, ig, jb = place_of(ahead)
-                if (ig, half) not in hs_banks:
-                    hs_banks[(ig, half)] = make_hs_bank(ig, half)

@@ -411,17 +411,6 @@ def tile_deepandwide_kernel(
             load_words(PASSES)
             load_small()
 
-        ctx.enter_context(
-            tc.manual_schedule(
-                engines={
-                    mybir.EngineType.DVE,
-                    mybir.EngineType.Activation,
-                    mybir.EngineType.Pool,
-                    mybir.EngineType.SP,
-                }
-            )
-        )
-
         todo = {}
 
         def at(step, work):

@@ -30,21 +30,24 @@ SHARED_TILES = 2
 VECTOR_GROUPS = SHARED_GROUP + 1
 SCALAR_GROUPS = I_GROUPS - SHARED_GROUP
 
-HALF_STEPS = VECTOR_GROUPS * J_BLOCKS
-STEPS = HALVES * HALF_STEPS
+HALF_PASSES = VECTOR_GROUPS * J_BLOCKS
 HALF_UNITS = SHARED_TILES + (SCALAR_GROUPS - 1) * TILES
 UNITS = HALVES * HALF_UNITS
 FIRST_SLOT = 1
-SLOT_STEPS = (15, 7)
+SLOT_PASSES = (15, 7)
 
 FLOPS = 2 * BATCH * FEATURES * FEATURES * WIDTH + 2 * BATCH * 2 * FEATURES * WIDTH
 
 
-def place_of(step):
-    half, rest = divmod(step, HALF_STEPS)
-    pair, rest = divmod(rest, 2 * J_BLOCKS)
-    jb, member = divmod(rest, 2)
-    return half, 2 * pair + member, jb
+def half_steps(half):
+    steps = []
+    for first in range(0, VECTOR_GROUPS, 2):
+        for jb in range(0, J_BLOCKS, 2):
+            if (half, first, jb) == (0, 0, 0):
+                steps.extend([(ig, one, 1) for one in (0, 1) for ig in (0, 1)])
+            else:
+                steps.extend([(ig, jb, 2) for ig in (first, first + 1)])
+    return steps
 
 
 def unit_of(unit):
@@ -58,7 +61,7 @@ def first_tile(ig):
 
 
 def slot_of(unit):
-    return FIRST_SLOT + unit * SLOT_STEPS[0] // SLOT_STEPS[1]
+    return FIRST_SLOT + unit * SLOT_PASSES[0] // SLOT_PASSES[1]
 
 
 def tile_deepandwide_kernel(
@@ -69,7 +72,8 @@ def tile_deepandwide_kernel(
         keep = ctx.enter_context(tc.tile_pool(name="keep", bufs=1))
         spread = ctx.enter_context(tc.tile_pool(name="spread", bufs=2))
         units = ctx.enter_context(tc.tile_pool(name="units", bufs=3))
-        stream = ctx.enter_context(tc.tile_pool(name="stream", bufs=8))
+        stream = ctx.enter_context(tc.tile_pool(name="stream", bufs=6))
+        product_pool = ctx.enter_context(tc.tile_pool(name="product_pool", bufs=4))
         psum_acc = ctx.enter_context(tc.psum_pool(name="psum_acc", bufs=1))
         psum_work = ctx.enter_context(tc.psum_pool(name="psum_work", bufs=4))
 
@@ -112,11 +116,13 @@ def tile_deepandwide_kernel(
             .rearrange("(ig s jb w) x -> ig jb s w x", ig=I_GROUPS, s=I_PER_PASS, jb=J_BLOCKS, w=BLOCK_P)
         )
         load_order = []
-        for step in range(HALF_STEPS):
-            load_order.append(place_of(step)[1:])
+        passes = 0
+        for ig, jb, count in half_steps(0):
+            load_order.extend([(ig, jb + more) for more in range(count)])
             for unit in range(HALF_UNITS):
-                if slot_of(unit + 2) == step:
-                    load_order.extend([(unit_of(unit)[1], jb) for jb in range(J_BLOCKS)])
+                if passes <= slot_of(unit + 2) < passes + count:
+                    load_order.extend([(unit_of(unit)[1], one) for one in range(J_BLOCKS)])
+            passes += count
 
         loaded = {}
 
@@ -178,7 +184,7 @@ def tile_deepandwide_kernel(
                 in_=rows.unsqueeze(1).to_broadcast([I_PER_PASS, BLOCK_P, HALF_B]),
             )
 
-        ht_rows = keep.tile([P, J_BLOCKS, HALVES, HALF_B * PACK], BF16)
+        ht_rows = keep.tile([P, HALVES, J_BLOCKS, HALF_B * PACK], BF16)
         ht_words = ht_sb[:].bitcast(F32)
 
         def widen_ht(jb, half, copy):
@@ -205,7 +211,7 @@ def tile_deepandwide_kernel(
                         )
                 columns = slice(pair * 2 * P * PACK, (pair + 1) * 2 * P * PACK)
                 copies[pair](
-                    out=ht_rows[:, jb, half, columns]
+                    out=ht_rows[:, half, jb, columns]
                     .bitcast(F32)
                     .rearrange("p (n c u) -> p n c u", n=2, u=2),
                     in_=bank[:].rearrange("p n u c -> p n c u"),
@@ -234,7 +240,7 @@ def tile_deepandwide_kernel(
         def fetch_ht(jb, half):
             rows = parked_ht[half][jb * BLOCK_P : (jb + 1) * BLOCK_P, :]
             nc.sync.dma_start(
-                out=ht_rows[:, jb, half, :].bitcast(F32),
+                out=ht_rows[:, half, jb, :].bitcast(F32),
                 in_=rows.unsqueeze(0).to_broadcast([I_PER_PASS, BLOCK_P, HALF_B * 2]),
             )
 
@@ -335,19 +341,20 @@ def tile_deepandwide_kernel(
             nc.vector.quantize_mx(out=v_words[:].bitcast(FP8X4), scales=v_scales[:], in_=operand[:])
             return v_words, v_scales
 
-        def multiply_step(half, ig, jb):
+        def multiply_step(half, ig, jb, count):
             first = first_tile(ig) * P
             rows = HALF_B - first
-            product = stream.tile([P, rows * PACK], BF16, align_bytes=64)
-            nc.vector.tensor_tensor(
-                out=product[:].rearrange("p (b u e) -> p b u e", u=2, e=2),
-                in0=ht_rows[:, jb, half, first * PACK :].rearrange("p (b u e) -> p b u e", u=2, e=2),
-                in1=hs_rows[:, ig, half, first * 2 :]
-                .rearrange("p (b e) -> p b e", e=2)
-                .unsqueeze(2)
-                .to_broadcast([P, rows, 2, 2]),
-                op=mybir.AluOpType.mult,
-            )
+            product = product_pool.tile([P, count * rows * PACK], BF16, align_bytes=64)
+            for one in range(count):
+                nc.vector.tensor_tensor(
+                    out=product[:].rearrange("p (j b u e) -> p j b u e", j=count, u=2, e=2)[:, one],
+                    in0=ht_rows[:, half, jb + one, first * PACK :].rearrange("p (b u e) -> p b u e", u=2, e=2),
+                    in1=hs_rows[:, ig, half, first * 2 :]
+                    .rearrange("p (b e) -> p b e", e=2)
+                    .unsqueeze(2)
+                    .to_broadcast([P, rows, 2, 2]),
+                    op=mybir.AluOpType.mult,
+                )
             return product
 
         acc = {}
@@ -413,8 +420,8 @@ def tile_deepandwide_kernel(
 
         todo = {}
 
-        def at(step, work):
-            todo.setdefault(step, []).append(work)
+        def at(passes, work):
+            todo.setdefault(passes, []).append(work)
 
         def second_half():
             prepare_units(1)
@@ -426,24 +433,28 @@ def tile_deepandwide_kernel(
                 fetch_hs(ig, 1)
 
         at(10, second_half)
-        at(HALF_STEPS - 5, make_bias_wide)
-        at(HALF_STEPS + 7, make_htT)
-        at(HALF_STEPS + 8, make_wlT)
+        at(HALF_PASSES - 4, make_bias_wide)
+        at(HALF_PASSES + 6, make_htT)
+        at(HALF_PASSES + 8, make_wlT)
         for pair in range(B_TILES // 2):
-            at(HALF_STEPS + 10 + 2 * pair, lambda pair=pair: deep_path(pair))
+            at(HALF_PASSES + 10 + 2 * pair, lambda pair=pair: deep_path(pair))
 
-        products = {}
+        steps = [(half, ig, jb, count) for half in range(HALVES) for ig, jb, count in half_steps(half)]
         by_batch = {}
         turned = {}
         ready = []
         open_half = 0
+        done = 0
+        waiting = None
 
-        for step in range(STEPS + 1):
-            for work in todo.get(step, []):
-                work()
+        for step in steps + [None]:
+            reached = range(done, done + (step[3] if step else 1))
+            for place in reached:
+                for work in todo.get(place, []):
+                    work()
             quantise_units = []
             for unit in range(UNITS + 2):
-                if slot_of(unit) != step:
+                if slot_of(unit) not in reached:
                     continue
                 if unit < UNITS:
                     by_batch[unit] = multiply_unit(unit)
@@ -451,18 +462,22 @@ def tile_deepandwide_kernel(
                     turned[unit - 1] = turn_unit(by_batch[unit - 1])
                 if unit - 2 >= 0:
                     quantise_units.append(unit - 2)
-            if step < STEPS:
-                half, ig, jb = place_of(step)
-                products[step] = multiply_step(half, ig, jb)
+            if step:
+                product = multiply_step(*step)
+                done += step[3]
             for unit in quantise_units:
                 half, ig, t = unit_of(unit)
                 quantised = quantise(turned[unit])
                 ready.append((half, [(quantised, jb, half, t, ig, jb) for jb in range(J_BLOCKS)]))
-            if step - 1 in products:
-                half, ig, jb = place_of(step - 1)
-                quantised = quantise(products[step - 1])
+            if waiting:
+                half, ig, jb, count = waiting[0]
+                quantised = quantise(waiting[1])
                 first = first_tile(ig)
-                ready.append((half, [(quantised, t - first, half, t, ig, jb) for t in range(first, TILES)]))
+                places = [(one, t) for one in range(count) for t in range(first, TILES)]
+                ready.append(
+                    (half, [(quantised, n, half, t, ig, jb + one) for n, (one, t) in enumerate(places)])
+                )
+            waiting = (step, product)
             held = []
             for half, passes in ready:
                 if half != open_half:

@@ -26,42 +26,38 @@ TILES = B_TILES // HALVES
 HALF_B = TILES * P
 
 SHARED_GROUP = 5
-SHARED_TILES = 2
+SHARED_TILES = (2, TILES)
 VECTOR_GROUPS = SHARED_GROUP + 1
 SCALAR_GROUPS = I_GROUPS - SHARED_GROUP
 
-HALF_PASSES = VECTOR_GROUPS * J_BLOCKS
-HALF_UNITS = SHARED_TILES + (SCALAR_GROUPS - 1) * TILES
-UNITS = HALVES * HALF_UNITS
-FIRST_SLOT = 1
-SLOT_PASSES = (15, 7)
+UNITS = [
+    (half, ig, t)
+    for half in range(HALVES)
+    for ig in range(SHARED_GROUP, I_GROUPS)
+    for t in range(SHARED_TILES[half] if ig == SHARED_GROUP else TILES)
+]
+VECTOR_UNITS = (0, 2)
+QUANT_LAG = 6
 
 FLOPS = 2 * BATCH * FEATURES * FEATURES * WIDTH + 2 * BATCH * 2 * FEATURES * WIDTH
 
 
+def first_tile(half, ig):
+    return SHARED_TILES[half] if ig == SHARED_GROUP else 0
+
+
 def half_steps(half):
+    groups = [ig for ig in range(VECTOR_GROUPS) if first_tile(half, ig) < TILES]
     steps = []
-    for first in range(0, VECTOR_GROUPS, 2):
+    for first in range(0, len(groups), 2):
+        pair = groups[first : first + 2]
         for jb in range(0, J_BLOCKS, 2):
-            if (half, first, jb) == (0, 0, 0):
-                steps.extend([(ig, one, 1) for one in (0, 1) for ig in (0, 1)])
-            else:
-                steps.extend([(ig, jb, 2) for ig in (first, first + 1)])
+            steps.extend([(ig, one, 1) for one in (jb, jb + 1) for ig in pair])
     return steps
 
 
-def unit_of(unit):
-    half, rest = divmod(unit, HALF_UNITS)
-    group, t = divmod(rest + TILES - SHARED_TILES, TILES)
-    return half, SHARED_GROUP + group, t - (TILES - SHARED_TILES if group == 0 else 0)
-
-
-def first_tile(ig):
-    return SHARED_TILES if ig == SHARED_GROUP else 0
-
-
-def slot_of(unit):
-    return FIRST_SLOT + unit * SLOT_PASSES[0] // SLOT_PASSES[1]
+def multiply_place(unit):
+    return 2 * unit - 5
 
 
 def tile_deepandwide_kernel(
@@ -72,7 +68,7 @@ def tile_deepandwide_kernel(
         keep = ctx.enter_context(tc.tile_pool(name="keep", bufs=1))
         spread = ctx.enter_context(tc.tile_pool(name="spread", bufs=2))
         units = ctx.enter_context(tc.tile_pool(name="units", bufs=3))
-        stream = ctx.enter_context(tc.tile_pool(name="stream", bufs=6))
+        stream = ctx.enter_context(tc.tile_pool(name="stream", bufs=7))
         product_pool = ctx.enter_context(tc.tile_pool(name="product_pool", bufs=4))
         psum_acc = ctx.enter_context(tc.psum_pool(name="psum_acc", bufs=1))
         psum_work = ctx.enter_context(tc.psum_pool(name="psum_work", bufs=4))
@@ -119,9 +115,9 @@ def tile_deepandwide_kernel(
         passes = 0
         for ig, jb, count in half_steps(0):
             load_order.extend([(ig, jb + more) for more in range(count)])
-            for unit in range(HALF_UNITS):
-                if passes <= slot_of(unit + 2) < passes + count:
-                    load_order.extend([(unit_of(unit)[1], one) for one in range(J_BLOCKS)])
+            for unit in range(len(UNITS)):
+                if passes <= multiply_place(unit) + 4 < passes + count:
+                    load_order.extend([(UNITS[unit][1], one) for one in range(J_BLOCKS)])
             passes += count
 
         loaded = {}
@@ -260,19 +256,27 @@ def tile_deepandwide_kernel(
                 out=hs_f32[:, tiles], in_=hs_sb[:, tiles, SHARED_GROUP * I_PER_PASS :]
             )
 
-        def multiply_unit(unit):
-            half, ig, t = unit_of(unit)
+        def multiply_unit(unit, by_batch, features):
+            half, ig, t = UNITS[unit]
             n = half * TILES + t
-            by_batch = units.tile([P, 2 * J_BLOCKS, I_PER_PASS, 2 * BLOCK_P], BF16)
-            for s in range(I_PER_PASS):
+            for s in features:
                 column = (ig - SHARED_GROUP) * I_PER_PASS + s
-                nc.scalar.activation(
-                    out=by_batch[:, :, s, :],
-                    in_=ht_sorted[:, n],
-                    func=mybir.ActivationFunctionType.Copy,
-                    scale=hs_f32[:, n, column : column + 1],
-                )
-            return by_batch
+                factor = hs_f32[:, n, column : column + 1]
+                if unit in VECTOR_UNITS:
+                    nc.vector.tensor_scalar(
+                        out=by_batch[:, :, s, :],
+                        in0=ht_sorted[:, n],
+                        scalar1=factor,
+                        scalar2=None,
+                        op0=mybir.AluOpType.mult,
+                    )
+                else:
+                    nc.scalar.activation(
+                        out=by_batch[:, :, s, :],
+                        in_=ht_sorted[:, n],
+                        func=mybir.ActivationFunctionType.Copy,
+                        scale=factor,
+                    )
 
         def turn_unit(by_batch):
             unit_product = units.tile([P, J_BLOCKS * P * PACK], BF16, align_bytes=64)
@@ -342,7 +346,7 @@ def tile_deepandwide_kernel(
             return v_words, v_scales
 
         def multiply_step(half, ig, jb, count):
-            first = first_tile(ig) * P
+            first = first_tile(half, ig) * P
             rows = HALF_B - first
             product = product_pool.tile([P, count * rows * PACK], BF16, align_bytes=64)
             for one in range(count):
@@ -390,23 +394,41 @@ def tile_deepandwide_kernel(
                     out=out_rows[:, n, WIDTH : 2 * WIDTH], in_=out_sb[:, n, WIDTH : 2 * WIDTH]
                 )
 
+        by_batch = {}
+        turned = {}
+
+        def begin_unit(unit):
+            products = units.tile([P, 2 * J_BLOCKS, I_PER_PASS, 2 * BLOCK_P], BF16)
+            by_batch[unit] = products
+
+        every = range(I_PER_PASS)
+        copies = (nc.vector.tensor_copy, nc.scalar.copy)
         with tc.manual_schedule():
             load_half(0)
             load_scales()
             load_words(4)
-            hs_bank = turn_hs(0)
             nc.vector.tensor_copy(
                 out=choose[:], in_=ident_bf16[:].unsqueeze(2).to_broadcast([P, FEATURES, BLOCK_P])
             )
-            ht_wide = widen_ht(0, 0, nc.vector.tensor_copy)
-            make_ht_rows(0, 0, ht_wide, (nc.vector.tensor_copy, nc.vector.tensor_copy))
-            make_hs_rows(0, 0)
-            park_ht(0)
-            ht_wide = widen_ht(1, 0, nc.vector.tensor_copy)
-            make_hs_rows(1, 0)
-            make_ht_rows(1, 0, ht_wide, (nc.scalar.copy, nc.scalar.copy))
-            park_hs(0, hs_bank)
+            hs_bank = turn_hs(0)
+            ht_wide = widen_ht(0, 0, copies[0])
             prepare_units(0)
+            begin_unit(0)
+            multiply_unit(0, by_batch[0], every)
+            begin_unit(1)
+            multiply_unit(1, by_batch[1], every[: I_PER_PASS // 2])
+            make_hs_rows(0, 0)
+            make_ht_rows(0, 0, ht_wide, (copies[0], copies[0]))
+            ht_wide = widen_ht(1, 0, copies[0])
+            park_ht(0)
+            turned[0] = turn_unit(by_batch[0])
+            make_hs_rows(1, 0)
+            make_ht_rows(1, 0, ht_wide, (copies[1], copies[1]))
+            park_hs(0, hs_bank)
+            multiply_unit(1, by_batch[1], every[I_PER_PASS // 2 :])
+            turned[1] = turn_unit(by_batch[1])
+            begin_unit(2)
+            multiply_unit(2, by_batch[2], every)
             load_words(2)
             for jb in range(2, J_BLOCKS):
                 fetch_ht(jb, 0)
@@ -430,22 +452,22 @@ def tile_deepandwide_kernel(
             for jb in range(J_BLOCKS):
                 fetch_ht(jb, 1)
             for ig in range(VECTOR_GROUPS):
-                fetch_hs(ig, 1)
+                if first_tile(1, ig) < TILES:
+                    fetch_hs(ig, 1)
 
         at(10, second_half)
-        at(HALF_PASSES - 4, make_bias_wide)
-        at(HALF_PASSES + 6, make_htT)
-        at(HALF_PASSES + 8, make_wlT)
+        at(20, make_bias_wide)
+        at(28, make_htT)
+        at(30, make_wlT)
         for pair in range(B_TILES // 2):
-            at(HALF_PASSES + 10 + 2 * pair, lambda pair=pair: deep_path(pair))
+            at(32 + 2 * pair, lambda pair=pair: deep_path(pair))
 
         steps = [(half, ig, jb, count) for half in range(HALVES) for ig, jb, count in half_steps(half)]
-        by_batch = {}
-        turned = {}
         ready = []
         open_half = 0
         done = 0
         waiting = None
+        closed = False
 
         for step in steps + [None]:
             reached = range(done, done + (step[3] if step else 1))
@@ -453,31 +475,34 @@ def tile_deepandwide_kernel(
                 for work in todo.get(place, []):
                     work()
             quantise_units = []
-            for unit in range(UNITS + 2):
-                if slot_of(unit) not in reached:
-                    continue
-                if unit < UNITS:
-                    by_batch[unit] = multiply_unit(unit)
-                if 0 <= unit - 1 < UNITS:
-                    turned[unit - 1] = turn_unit(by_batch[unit - 1])
-                if unit - 2 >= 0:
-                    quantise_units.append(unit - 2)
+            for unit in range(len(UNITS)):
+                if multiply_place(unit) in reached:
+                    begin_unit(unit)
+                    multiply_unit(unit, by_batch[unit], every)
+            for unit in range(len(UNITS)):
+                if multiply_place(unit) + 2 in reached:
+                    turned[unit] = turn_unit(by_batch[unit])
+                if multiply_place(unit) + QUANT_LAG in reached:
+                    quantise_units.append(unit)
             if step:
                 product = multiply_step(*step)
                 done += step[3]
             for unit in quantise_units:
-                half, ig, t = unit_of(unit)
+                half, ig, t = UNITS[unit]
                 quantised = quantise(turned[unit])
                 ready.append((half, [(quantised, jb, half, t, ig, jb) for jb in range(J_BLOCKS)]))
             if waiting:
                 half, ig, jb, count = waiting[0]
                 quantised = quantise(waiting[1])
-                first = first_tile(ig)
+                first = first_tile(half, ig)
                 places = [(one, t) for one in range(count) for t in range(first, TILES)]
                 ready.append(
                     (half, [(quantised, n, half, t, ig, jb + one) for n, (one, t) in enumerate(places)])
                 )
             waiting = (step, product)
+            if closed:
+                store_half(open_half)
+                open_half += 1
             held = []
             for half, passes in ready:
                 if half != open_half:
@@ -486,6 +511,5 @@ def tile_deepandwide_kernel(
                 for one in passes:
                     contract(*one)
             ready = held
-            if all([added.get((open_half, t), 0) == PASSES for t in range(TILES)]):
-                store_half(open_half)
-                open_half += 1
+            closed = all([added.get((open_half, t), 0) == PASSES for t in range(TILES)])
+        store_half(open_half)

from contextlib import ExitStack

import concourse.mybir as mybir
from concourse.masks import make_identity

BF16 = mybir.dt.bfloat16
F32 = mybir.dt.float32
I32 = mybir.dt.int32
U32 = mybir.dt.uint32
U8 = mybir.dt.uint8
FP8X4 = mybir.dt.float8_e4m3fn_x4

P = 128
BATCH = 1024
FEATURES = 128
WIDTH = 256
PACK = 4
BLOCK_P = 8
I_PER_PASS = P // BLOCK_P
I_GROUPS = FEATURES // I_PER_PASS
J_BLOCKS = FEATURES // (BLOCK_P * PACK)
PASSES = I_GROUPS * J_BLOCKS
B_TILES = BATCH // P
HALVES = 2
TILES = B_TILES // HALVES
HALF_B = TILES * P

SHARED_GROUP = 5
SHARED_TILES = (2, TILES)
VECTOR_GROUPS = SHARED_GROUP + 1
SCALAR_GROUPS = I_GROUPS - SHARED_GROUP

UNITS = [
    (half, ig, t)
    for half in range(HALVES)
    for ig in range(SHARED_GROUP, I_GROUPS)
    for t in range(SHARED_TILES[half] if ig == SHARED_GROUP else TILES)
]
VECTOR_UNITS = (0, 2)
QUANT_LAG = 6

FLOPS = 2 * BATCH * FEATURES * FEATURES * WIDTH + 2 * BATCH * 2 * FEATURES * WIDTH


def first_tile(half, ig):
    return SHARED_TILES[half] if ig == SHARED_GROUP else 0


def half_steps(half):
    groups = [ig for ig in range(VECTOR_GROUPS) if first_tile(half, ig) < TILES]
    steps = []
    for first in range(0, len(groups), 2):
        pair = groups[first : first + 2]
        for jb in range(0, J_BLOCKS, 2):
            steps.extend([(ig, one, 1) for one in (jb, jb + 1) for ig in pair])
    return steps


def multiply_place(unit):
    return 2 * unit - 5


def tile_deepandwide_kernel(
    tc, hspatial, htext, W_L, b_L, W_L2_words, W_L2_scales, b_L2, out
):
    nc = tc.nc
    with ExitStack() as ctx:
        keep = ctx.enter_context(tc.tile_pool(name="keep", bufs=1))
        spread = ctx.enter_context(tc.tile_pool(name="spread", bufs=2))
        units = ctx.enter_context(tc.tile_pool(name="units", bufs=3))
        stream = ctx.enter_context(tc.tile_pool(name="stream", bufs=7))
        product_pool = ctx.enter_context(tc.tile_pool(name="product_pool", bufs=4))
        psum_acc = ctx.enter_context(tc.psum_pool(name="psum_acc", bufs=1))
        psum_work = ctx.enter_context(tc.psum_pool(name="psum_work", bufs=4))

        ident_bf16 = keep.tile([P, P], BF16)
        make_identity(nc, ident_bf16[:])
        ident_f32 = keep.tile([P, P], F32)
        make_identity(nc, ident_f32[:])
        ones = keep.tile([P, P], BF16)
        nc.gpsimd.memset(ones[:], 1.0)

        hs_sb = keep.tile([P, B_TILES, FEATURES], BF16)
        ht_sb = keep.tile([P, B_TILES, FEATURES], BF16)
        hs_dram = hspatial.rearrange("(c n) i -> c n i", n=B_TILES)
        ht_dram = htext.rearrange("(c n) j -> c n j", n=B_TILES)

        def load_half(half):
            tiles = slice(half * TILES, (half + 1) * TILES)
            nc.sync.dma_start(out=ht_sb[:, tiles], in_=ht_dram[:, tiles])
            nc.sync.dma_start(out=hs_sb[:, tiles], in_=hs_dram[:, tiles])

        w_scales = keep.tile([P, I_GROUPS, J_BLOCKS, WIDTH], U8, align_bytes=64)
        scale_rows = (
            W_L2_scales.rearrange("g q n -> (g q) n")
            .rearrange("(ig Q r jb) n -> Q r ig (jb n)", ig=I_GROUPS, Q=4, r=4, jb=J_BLOCKS)
            .bitcast(I32)
        )

        def load_scales():
            nc.vector.memset(w_scales[:].rearrange("p a b n -> p (a b n)").bitcast(I32), 0)
            for Q in range(4):
                nc.sync.dma_start(
                    out=w_scales[32 * Q : 32 * Q + 4].rearrange("r a b n -> r a (b n)").bitcast(I32),
                    in_=scale_rows[Q],
                )

        w_words = keep.tile([P, I_GROUPS, J_BLOCKS, WIDTH], U32, align_bytes=64)
        word_rows = (
            W_L2_words.rearrange("g p n t -> (g p) (n t)")
            .bitcast(I32)
            .rearrange("(ig s jb w) x -> ig jb s w x", ig=I_GROUPS, s=I_PER_PASS, jb=J_BLOCKS, w=BLOCK_P)
        )
        load_order = []
        passes = 0
        for ig, jb, count in half_steps(0):
            load_order.extend([(ig, jb + more) for more in range(count)])
            for unit in range(len(UNITS)):
                if passes <= multiply_place(unit) + 4 < passes + count:
                    load_order.extend([(UNITS[unit][1], one) for one in range(J_BLOCKS)])
            passes += count

        loaded = {}

        def load_words(count):
            goal = len(loaded) + count
            for ig, jb in load_order:
                if (ig, jb) not in loaded and len(loaded) < goal:
                    nc.sync.dma_start(out=w_words[:, ig, jb, :].bitcast(I32), in_=word_rows[ig, jb])
                    loaded[(ig, jb)] = True

        wl_sb = keep.tile([P, 2, 2 * FEATURES], BF16)
        bias_rows = keep.tile([P, 2 * WIDTH], BF16)

        def load_small():
            nc.vector.memset(bias_rows[:].bitcast(I32), 0)
            nc.sync.dma_start(out=wl_sb[:], in_=W_L.rearrange("(t o) k -> o t k", t=2))
            nc.sync.dma_start(out=bias_rows[0:1, 0:WIDTH], in_=b_L.unsqueeze(0))
            nc.sync.dma_start(out=bias_rows[0:1, WIDTH : 2 * WIDTH], in_=b_L2.unsqueeze(0))

        choose = keep.tile([P, FEATURES, BLOCK_P], BF16)

        hsT = keep.tile([P, B_TILES, P], BF16)
        hs_pairs = keep.tile([P, B_TILES, P, 2], BF16)
        hs_rows = keep.tile([P, VECTOR_GROUPS, HALVES, HALF_B * 2], BF16)

        def turn_hs(half):
            bank = psum_work.tile([P, TILES, P], BF16, tag="work")
            for t in range(TILES):
                nc.tensor.transpose(bank[:, t, :], hs_sb[:, half * TILES + t, :], ident_bf16[:])
            nc.scalar.copy(out=hsT[:, half * TILES : (half + 1) * TILES], in_=bank[:])
            return bank

        def make_hs_rows(ig, half):
            bank = psum_work.tile([P, 2, 2, P, 2], BF16, tag="work")
            for k in range(2):
                first = half * TILES + 2 * k
                nc.tensor.matmul(
                    bank[:, k],
                    lhsT=choose[:, ig * I_PER_PASS : (ig + 1) * I_PER_PASS, :].rearrange("p s w -> p (s w)"),
                    rhs=hsT[:, first : first + 2, :].unsqueeze(3).to_broadcast([P, 2, P, 2]),
                    start=True,
                    stop=True,
                )
            nc.scalar.copy(out=hs_rows[:, ig, half, :], in_=bank[:].rearrange("p k n c e -> p (k n c e)"))

        parked_hs = [out.rearrange("(i r) f -> i r f", r=B_TILES)[:, 6 + half, :] for half in range(HALVES)]

        def park_hs(half, bank):
            tiles = slice(half * TILES, (half + 1) * TILES)
            nc.scalar.copy(out=hs_pairs[:, tiles], in_=bank[:].unsqueeze(3).to_broadcast([P, TILES, P, 2]))
            nc.scalar.dma_start(
                out=parked_hs[half], in_=hs_pairs[:, tiles].rearrange("p n c e -> p (n c e)").bitcast(F32)
            )

        def fetch_hs(ig, half):
            rows = parked_hs[half][ig * I_PER_PASS : (ig + 1) * I_PER_PASS, :]
            nc.sync.dma_start(
                out=hs_rows[:, ig, half, :].bitcast(F32),
                in_=rows.unsqueeze(1).to_broadcast([I_PER_PASS, BLOCK_P, HALF_B]),
            )

        ht_rows = keep.tile([P, HALVES, J_BLOCKS, HALF_B * PACK], BF16)
        ht_words = ht_sb[:].bitcast(F32)

        def widen_ht(jb, half, copy):
            ht_wide = spread.tile([P, 2, TILES, I_PER_PASS, BLOCK_P], F32)
            for u in range(2):
                words = slice(2 * BLOCK_P * jb + u, 2 * BLOCK_P * (jb + 1), 2)
                copy(
                    out=ht_wide[:, u],
                    in_=ht_words[:, half * TILES : (half + 1) * TILES, words]
                    .unsqueeze(2)
                    .to_broadcast([P, TILES, I_PER_PASS, BLOCK_P]),
                )
            return ht_wide

        def make_ht_rows(jb, half, ht_wide, copies):
            for pair in range(TILES // 2):
                bank = psum_acc.tile([P, 2, 2, P], F32, name="acc%d" % (2 * jb + pair))
                for n in range(2):
                    for u in range(2):
                        nc.tensor.transpose(
                            bank[:, n, u, :],
                            ht_wide[:, u, 2 * pair + n].rearrange("p s w -> p (s w)"),
                            ident_f32[:],
                        )
                columns = slice(pair * 2 * P * PACK, (pair + 1) * 2 * P * PACK)
                copies[pair](
                    out=ht_rows[:, half, jb, columns]
                    .bitcast(F32)
                    .rearrange("p (n c u) -> p n c u", n=2, u=2),
                    in_=bank[:].rearrange("p n u c -> p n c u"),
                )

        parked_ht = [
            out.rearrange("(x r) f -> x r f", r=B_TILES)[: J_BLOCKS * BLOCK_P, 2 + 2 * half : 4 + 2 * half, :]
            .rearrange("x r f -> x (r f)")
            for half in range(HALVES)
        ]

        def park_ht(half):
            bank = psum_work.tile([P, 2, P], F32, tag="work")
            words = ht_words[:, half * TILES : (half + 1) * TILES, :].rearrange("p n x -> p (n x)")
            for u in range(2):
                nc.tensor.transpose(bank[:, u, :], words[:, u::2], ident_f32[:])
            turned_ht = spread.tile([P, P, 2], F32)
            nc.scalar.copy(out=turned_ht[:], in_=bank[:].rearrange("p u c -> p c u"))
            rows = J_BLOCKS * BLOCK_P
            for n in range(TILES):
                nc.scalar.dma_start(
                    out=parked_ht[half][:, n * 2 * P : (n + 1) * 2 * P],
                    in_=turned_ht[n * rows : (n + 1) * rows].rearrange("p c u -> p (c u)"),
                )

        def fetch_ht(jb, half):
            rows = parked_ht[half][jb * BLOCK_P : (jb + 1) * BLOCK_P, :]
            nc.sync.dma_start(
                out=ht_rows[:, half, jb, :].bitcast(F32),
                in_=rows.unsqueeze(0).to_broadcast([I_PER_PASS, BLOCK_P, HALF_B * 2]),
            )

        ht_sorted = keep.tile([P, B_TILES, 2 * J_BLOCKS, 2 * BLOCK_P], BF16)
        hs_f32 = keep.tile([P, B_TILES, SCALAR_GROUPS * I_PER_PASS], F32)

        def prepare_units(half):
            tiles = slice(half * TILES, (half + 1) * TILES)
            nc.vector.tensor_copy(
                out=ht_sorted[:, tiles]
                .rearrange("p n a x -> p (n a x)")
                .bitcast(F32)
                .rearrange("p (m u w) -> p m u w", u=2, w=BLOCK_P),
                in_=ht_words[:, tiles].rearrange("p n (jb w u) -> p (n jb) u w", w=BLOCK_P, u=2),
            )
            nc.vector.tensor_copy(
                out=hs_f32[:, tiles], in_=hs_sb[:, tiles, SHARED_GROUP * I_PER_PASS :]
            )

        def multiply_unit(unit, by_batch, features):
            half, ig, t = UNITS[unit]
            n = half * TILES + t
            for s in features:
                column = (ig - SHARED_GROUP) * I_PER_PASS + s
                factor = hs_f32[:, n, column : column + 1]
                if unit in VECTOR_UNITS:
                    nc.vector.tensor_scalar(
                        out=by_batch[:, :, s, :],
                        in0=ht_sorted[:, n],
                        scalar1=factor,
                        scalar2=None,
                        op0=mybir.AluOpType.mult,
                    )
                else:
                    nc.scalar.activation(
                        out=by_batch[:, :, s, :],
                        in_=ht_sorted[:, n],
                        func=mybir.ActivationFunctionType.Copy,
                        scale=factor,
                    )

        def turn_unit(by_batch):
            unit_product = units.tile([P, J_BLOCKS * P * PACK], BF16, align_bytes=64)
            for pair in range(J_BLOCKS // 2):
                bank = psum_work.tile([P, 2, 2, P], F32, tag="work")
                for j in range(2):
                    for u in range(2):
                        nc.tensor.transpose(
                            bank[:, j, u, :],
                            by_batch[:, 4 * pair + 2 * j + u].rearrange("p s x -> p (s x)").bitcast(F32),
                            ident_f32[:],
                        )
                columns = slice(pair * 2 * P * PACK, (pair + 1) * 2 * P * PACK)
                nc.scalar.copy(
                    out=unit_product[:, columns]
                    .bitcast(F32)
                    .rearrange("p (j c u) -> p j c u", j=2, u=2),
                    in_=bank[:].rearrange("p j u c -> p j c u"),
                )
            return unit_product

        out_sb = keep.tile([P, B_TILES, 2 * WIDTH], F32)
        out_rows = out.rearrange("(c n) f -> c n f", n=B_TILES)
        htT = keep.tile([P, B_TILES, P], BF16)
        wlT = keep.tile([P, 2, WIDTH], BF16)
        bias_wide = keep.tile([P, WIDTH], F32)

        def make_bias_wide():
            bank = psum_work.tile([P, WIDTH], F32, tag="work")
            nc.tensor.matmul(
                bank[:], lhsT=ones[:], rhs=bias_rows[:, WIDTH : 2 * WIDTH], start=True, stop=True
            )
            nc.scalar.copy(out=bias_wide[:], in_=bank[:])

        def make_htT():
            bank = psum_work.tile([P, B_TILES, P], BF16, tag="work")
            for n in range(B_TILES):
                nc.tensor.transpose(bank[:, n, :], ht_sb[:, n, :], ident_bf16[:])
            nc.scalar.copy(out=htT[:], in_=bank[:])

        def make_wlT():
            bank = psum_work.tile([P, 2, WIDTH], BF16, tag="work")
            for kh in range(2):
                for t in range(2):
                    nc.tensor.transpose(
                        bank[:, kh, t * P : (t + 1) * P], wl_sb[:, t, kh * P : (kh + 1) * P], ident_bf16[:]
                    )
            nc.scalar.copy(out=wlT[:], in_=bank[:])

        def deep_path(pair):
            bank = psum_work.tile([P, 2, WIDTH], F32, tag="work")
            for k in range(2):
                n = 2 * pair + k
                nc.tensor.matmul(bank[:, k, :], lhsT=hsT[:, n, :], rhs=wlT[:, 0, :], start=True, stop=False)
                nc.tensor.matmul(bank[:, k, :], lhsT=htT[:, n, :], rhs=wlT[:, 1, :], start=False, stop=False)
                nc.tensor.matmul(bank[:, k, :], lhsT=ones[:], rhs=bias_rows[:, 0:WIDTH], start=False, stop=True)
            nc.scalar.copy(out=out_sb[:, 2 * pair : 2 * pair + 2, 0:WIDTH], in_=bank[:])
            nc.sync.dma_start(
                out=out_rows[:, 2 * pair : 2 * pair + 2, 0:WIDTH],
                in_=out_sb[:, 2 * pair : 2 * pair + 2, 0:WIDTH],
            )

        def quantise(operand):
            v_words = stream.tile([P, operand.shape[1] // PACK], U32, align_bytes=64)
            v_scales = stream.tile([P, operand.shape[1] // PACK], U8, align_bytes=64)
            nc.vector.quantize_mx(out=v_words[:].bitcast(FP8X4), scales=v_scales[:], in_=operand[:])
            return v_words, v_scales

        def multiply_step(half, ig, jb, count):
            first = first_tile(half, ig) * P
            rows = HALF_B - first
            product = product_pool.tile([P, count * rows * PACK], BF16, align_bytes=64)
            for one in range(count):
                nc.vector.tensor_tensor(
                    out=product[:].rearrange("p (j b u e) -> p j b u e", j=count, u=2, e=2)[:, one],
                    in0=ht_rows[:, half, jb + one, first * PACK :].rearrange("p (b u e) -> p b u e", u=2, e=2),
                    in1=hs_rows[:, ig, half, first * 2 :]
                    .rearrange("p (b e) -> p b e", e=2)
                    .unsqueeze(2)
                    .to_broadcast([P, rows, 2, 2]),
                    op=mybir.AluOpType.mult,
                )
            return product

        acc = {}
        added = {}

        def contract(quantised, piece, half, t, ig, jb):
            v_words, v_scales = quantised
            count = added.get((half, t), 0)
            if count == 0:
                acc[(half, t)] = psum_acc.tile([P, WIDTH], F32, name="acc%d" % t)
            columns = slice(piece * P, (piece + 1) * P)
            nc.tensor.matmul_mx(
                out=acc[(half, t)][:],
                lhsT=v_words[:, columns].bitcast(FP8X4),
                lhsT_scale=v_scales[:, columns],
                rhs=w_words[:, ig, jb, :].bitcast(FP8X4),
                rhs_scale=w_scales[:, ig, jb, :],
                start=count == 0,
                stop=count == PASSES - 1,
            )
            added[(half, t)] = count + 1

        def store_half(half):
            for t in range(TILES):
                n = half * TILES + t
                nc.vector.tensor_tensor(
                    out=out_sb[:, n, WIDTH : 2 * WIDTH],
                    in0=acc[(half, t)][:],
                    in1=bias_wide[:],
                    op=mybir.AluOpType.add,
                )
                nc.sync.dma_start(
                    out=out_rows[:, n, WIDTH : 2 * WIDTH], in_=out_sb[:, n, WIDTH : 2 * WIDTH]
                )

        by_batch = {}
        turned = {}

        def begin_unit(unit):
            products = units.tile([P, 2 * J_BLOCKS, I_PER_PASS, 2 * BLOCK_P], BF16)
            by_batch[unit] = products

        every = range(I_PER_PASS)
        copies = (nc.vector.tensor_copy, nc.scalar.copy)
        with tc.manual_schedule():
            load_half(0)
            load_scales()
            load_words(4)
            nc.vector.tensor_copy(
                out=choose[:], in_=ident_bf16[:].unsqueeze(2).to_broadcast([P, FEATURES, BLOCK_P])
            )
            hs_bank = turn_hs(0)
            ht_wide = widen_ht(0, 0, copies[0])
            prepare_units(0)
            begin_unit(0)
            multiply_unit(0, by_batch[0], every)
            begin_unit(1)
            multiply_unit(1, by_batch[1], every[: I_PER_PASS // 2])
            make_hs_rows(0, 0)
            make_ht_rows(0, 0, ht_wide, (copies[0], copies[0]))
            ht_wide = widen_ht(1, 0, copies[0])
            park_ht(0)
            turned[0] = turn_unit(by_batch[0])
            make_hs_rows(1, 0)
            make_ht_rows(1, 0, ht_wide, (copies[1], copies[1]))
            park_hs(0, hs_bank)
            multiply_unit(1, by_batch[1], every[I_PER_PASS // 2 :])
            turned[1] = turn_unit(by_batch[1])
            begin_unit(2)
            multiply_unit(2, by_batch[2], every)
            load_words(2)
            for jb in range(2, J_BLOCKS):
                fetch_ht(jb, 0)
                load_words(2)
            for ig in range(2, VECTOR_GROUPS):
                fetch_hs(ig, 0)
                load_words(4)
            load_half(1)
            load_words(PASSES)
            load_small()

        todo = {}

        def at(passes, work):
            todo.setdefault(passes, []).append(work)

        def second_half():
            prepare_units(1)
            park_ht(1)
            park_hs(1, turn_hs(1))
            for jb in range(J_BLOCKS):
                fetch_ht(jb, 1)
            for ig in range(VECTOR_GROUPS):
                if first_tile(1, ig) < TILES:
                    fetch_hs(ig, 1)

        at(10, second_half)
        at(20, make_bias_wide)
        at(28, make_htT)
        at(30, make_wlT)
        for pair in range(B_TILES // 2):
            at(32 + 2 * pair, lambda pair=pair: deep_path(pair))

        steps = [(half, ig, jb, count) for half in range(HALVES) for ig, jb, count in half_steps(half)]
        ready = []
        open_half = 0
        done = 0
        waiting = None
        closed = False

        for step in steps + [None]:
            reached = range(done, done + (step[3] if step else 1))
            for place in reached:
                for work in todo.get(place, []):
                    work()
            quantise_units = []
            for unit in range(len(UNITS)):
                if multiply_place(unit) in reached:
                    begin_unit(unit)
                    multiply_unit(unit, by_batch[unit], every)
            for unit in range(len(UNITS)):
                if multiply_place(unit) + 2 in reached:
                    turned[unit] = turn_unit(by_batch[unit])
                if multiply_place(unit) + QUANT_LAG in reached:
                    quantise_units.append(unit)
            if step:
                product = multiply_step(*step)
                done += step[3]
            for unit in quantise_units:
                half, ig, t = UNITS[unit]
                quantised = quantise(turned[unit])
                ready.append((half, [(quantised, jb, half, t, ig, jb) for jb in range(J_BLOCKS)]))
            if waiting:
                half, ig, jb, count = waiting[0]
                quantised = quantise(waiting[1])
                first = first_tile(half, ig)
                places = [(one, t) for one in range(count) for t in range(first, TILES)]
                ready.append(
                    (half, [(quantised, n, half, t, ig, jb + one) for n, (one, t) in enumerate(places)])
                )
            waiting = (step, product)
            if closed:
                store_half(open_half)
                open_half += 1
            held = []
            for half, passes in ready:
                if half != open_half:
                    held.append((half, passes))
                    continue
                for one in passes:
                    contract(*one)
            ready = held
            closed = all([added.get((open_half, t), 0) == PASSES for t in range(TILES)])
        store_half(open_half)
